import numpy as np
import ml_dtypes


def mxq(x, axis, fmt="e4m3"):
    dtype, down = {"e4m3": (ml_dtypes.float8_e4m3fn, 7), "e5m2": (ml_dtypes.float8_e5m2, 14)}[fmt]
    v = np.moveaxis(np.asarray(x, np.float32).astype(ml_dtypes.bfloat16).astype(np.float64), axis, -1)
    blocks = v.reshape(v.shape[:-1] + (-1, 32))
    amax = np.abs(blocks).max(-1, keepdims=True)
    byte = np.maximum(np.where(amax > 0, np.frexp(amax)[1] - 1 + 127, 0) - down, 1)
    scale = np.exp2(byte - 127.0)
    codes = (blocks / scale).astype(np.float32).astype(dtype).astype(np.float64)
    return np.moveaxis((codes * scale).reshape(v.shape), -1, axis)


WIDE = False


def mx_kscale(k):
    if not WIDE:
        return np.ones(k)
    levels = np.array([10, -10, 5, -5, 0])
    a = np.random.permutation(np.resize(levels, k // 512 * 4)).reshape(k // 512, 4)
    idx = np.arange(k)
    return np.exp2(a[idx // 512, idx % 128 // 32])


BF16 = ml_dtypes.bfloat16


def bf(x):
    return np.asarray(x, np.float32).astype(BF16)


def f64(x):
    return np.asarray(x).astype(np.float64)


E2M1 = np.array([0.0, 0.5, 1.0, 1.5, 2.0, 3.0, 4.0, 6.0, -0.0, -0.5, -1.0, -1.5, -2.0, -3.0, -4.0, -6.0])


def pack_weight(w, fmt):
    k, n = w.shape
    w = f64(bf(w)).reshape(k // 32, 32, n)
    amax = np.abs(w).max(1)
    if fmt == "e4m3":
        byte = np.frexp(amax)[1] - 1 + 127 - 7
    else:
        mant, ex = np.frexp(amax / 6.0)
        byte = np.where(mant > 0.5, ex, ex - 1) + 127
    byte = np.clip(np.where(amax > 0, byte, 1), 1, 254)
    scaled = (w * np.exp2(127.0 - byte)[:, None, :]).reshape(k, n).astype(np.float32)
    by_word = np.ascontiguousarray(scaled.reshape(k // 512, 128, 4, n).transpose(0, 1, 3, 2))
    if fmt == "e4m3":
        words = by_word.astype(ml_dtypes.float8_e4m3fn).view(np.uint8)
    else:
        c = by_word.astype(ml_dtypes.float4_e2m1fn).view(np.uint8) & 0xF
        words = c[..., 0::2] | (c[..., 1::2] << 4)
    return np.ascontiguousarray(words), np.ascontiguousarray(byte.astype(np.uint8).reshape(k // 512, 16, n))


def unpack_weight(words, scales, fmt):
    g, p, n, _ = words.shape
    if fmt == "e4m3":
        vals = np.ascontiguousarray(words).view(ml_dtypes.float8_e4m3fn).astype(np.float64)
    else:
        nib = np.empty((g, p, n, 4), np.uint8)
        nib[..., 0::2] = words & 0xF
        nib[..., 1::2] = words >> 4
        vals = E2M1[nib]
    vals = vals * np.repeat(np.exp2(scales.astype(np.float64) - 127.0), 8, axis=1)[..., None]
    return vals.transpose(0, 1, 3, 2).reshape(g * 512, n)


B, S, D, E = 2, 128, 16384, 128
EPS = 1e-5
FMT = "e4m3"


def layer_norm(x, g, b):
    mu = x.mean(-1, keepdims=True)
    var = np.square(x - mu).mean(-1, keepdims=True)
    return (x - mu) / np.sqrt(var + EPS) * g + b


def setup_inputs():
    s = mx_kscale(D)

    def stream():
        return bf(np.random.standard_normal((B, S, D)) + 0.5 * np.random.standard_normal((B, S, 1)))

    def gain():
        return bf((1.0 + 0.1 * np.random.standard_normal(D)) * s)

    def shift():
        return bf(0.1 * np.random.standard_normal(D) * s)

    def weight(a):
        w = np.random.standard_normal((E, D)) * a / np.sqrt(D) / s[None, :]
        return pack_weight(np.ascontiguousarray(w.T), FMT)

    def bias():
        return bf(0.2 * np.random.standard_normal(E))

    text = stream()
    img = stream()
    ln_t_g = gain()
    ln_t_b = shift()
    ln_i_g = gain()
    ln_i_b = shift()
    Wq_words, Wq_scales = weight(1.5)
    bq = bias()
    Wkt_words, Wkt_scales = weight(1.5)
    bkt = bias()
    Wvt_words, Wvt_scales = weight(1.0)
    bvt = bias()
    Wki_words, Wki_scales = weight(1.5)
    bki = bias()
    Wvi_words, Wvi_scales = weight(1.0)
    bvi = bias()
    return {"text": text, "img": img,
            "ln_t_g": ln_t_g, "ln_t_b": ln_t_b, "ln_i_g": ln_i_g, "ln_i_b": ln_i_b,
            "Wq_words": Wq_words, "Wq_scales": Wq_scales, "bq": bq,
            "Wkt_words": Wkt_words, "Wkt_scales": Wkt_scales, "bkt": bkt,
            "Wvt_words": Wvt_words, "Wvt_scales": Wvt_scales, "bvt": bvt,
            "Wki_words": Wki_words, "Wki_scales": Wki_scales, "bki": bki,
            "Wvi_words": Wvi_words, "Wvi_scales": Wvi_scales, "bvi": bvi}


def reference(text, img, ln_t_g, ln_t_b, ln_i_g, ln_i_b, Wq_words, Wq_scales, bq, Wkt_words, Wkt_scales, bkt, Wvt_words, Wvt_scales, bvt, Wki_words, Wki_scales, bki, Wvi_words, Wvi_scales, bvi):
    tn = mxq(layer_norm(f64(text), f64(ln_t_g), f64(ln_t_b)), 2, "e4m3")
    im = mxq(layer_norm(f64(img), f64(ln_i_g), f64(ln_i_b)), 2, "e4m3")
    wq = unpack_weight(Wq_words, Wq_scales, FMT)
    q = np.concatenate([(tn @ wq), (im @ wq)], 0) + f64(bq)
    k = np.concatenate([(tn @ unpack_weight(Wkt_words, Wkt_scales, FMT)) + f64(bkt), (im @ unpack_weight(Wki_words, Wki_scales, FMT)) + f64(bki)], 0)
    v = np.concatenate([(tn @ unpack_weight(Wvt_words, Wvt_scales, FMT)) + f64(bvt), (im @ unpack_weight(Wvi_words, Wvi_scales, FMT)) + f64(bvi)], 0)
    return q, k, v

@@ -1,0 +1,342 @@
+from contextlib import ExitStack
+
+import concourse.mybir as mybir
+from concourse.masks import make_identity
+
+F32 = mybir.dt.float32
+BF16 = mybir.dt.bfloat16
+I32 = mybir.dt.int32
+U32 = mybir.dt.uint32
+U8 = mybir.dt.uint8
+FP8X4 = mybir.dt.float8_e4m3fn_x4
+ACT = mybir.ActivationFunctionType
+ALU = mybir.AluOpType
+
+P = 128
+PACK = 4
+K_PASS = P * PACK
+D = 16384
+E = 128
+EPS = 1e-5
+STREAMS = 2
+TILES = 2
+ROWS = TILES * P
+GROUPS = D // K_PASS
+
+CHUNK = 2048
+CHUNKS = D // CHUNK
+X_BUFS = 12
+STAT_BLOCK = 512
+BLOCKS = CHUNK // STAT_BLOCK
+
+SCALAR_CHUNKS = [c for c in range(CHUNKS) if c % 3 == 0]
+VECTOR_CHUNKS = [c for c in range(CHUNKS) if c % 3 != 0]
+VECTOR_TUPLES = 2 * BLOCKS * len(VECTOR_CHUNKS)
+TUPLES = VECTOR_TUPLES + len(SCALAR_CHUNKS)
+VECTOR_JOBS = TILES * BLOCKS * len(VECTOR_CHUNKS)
+SCALAR_JOBS = 2 * TILES * len(SCALAR_CHUNKS)
+
+ROUND_GROUPS = 2
+ROUND_COLS = ROUND_GROUPS * K_PASS
+ROUNDS = GROUPS // ROUND_GROUPS
+ROUNDS_PER_CHUNK = CHUNK // ROUND_COLS
+W_GROUPS = 4
+W_TILES = GROUPS // W_GROUPS
+W_BUFS = 4
+ROUNDS_PER_W = W_GROUPS // ROUND_GROUPS
+
+FLOPS = 2 * 3 * STREAMS * ROWS * D * E
+
+
+def tile_modalityadaptivemodule_pa_k_kernel(
+    tc,
+    text, img, ln_t_g, ln_t_b, ln_i_g, ln_i_b,
+    Wq_words, Wq_scales, bq,
+    Wkt_words, Wkt_scales, bkt,
+    Wvt_words, Wvt_scales, bvt,
+    Wki_words, Wki_scales, bki,
+    Wvi_words, Wvi_scales, bvi,
+    out_0, out_1, out_2,
+):
+    nc = tc.nc
+    streams = (text, img)
+    words_of = ((Wq_words, Wkt_words, Wvt_words), (Wq_words, Wki_words, Wvi_words))
+    scales_of = ((Wq_scales, Wkt_scales, Wvt_scales), (Wq_scales, Wki_scales, Wvi_scales))
+    outs = (out_0, out_1, out_2)
+
+    with ExitStack() as ctx:
+        const = ctx.enter_context(tc.tile_pool(name="const", bufs=1))
+        x_pool = ctx.enter_context(tc.tile_pool(name="x", bufs=X_BUFS))
+        w_pool = ctx.enter_context(tc.tile_pool(name="w", bufs=W_BUFS))
+        work = ctx.enter_context(tc.tile_pool(name="work", bufs=2))
+        mx_pool = ctx.enter_context(tc.tile_pool(name="mx", bufs=3))
+        turn_psum = ctx.enter_context(tc.psum_pool(name="turn", bufs=4))
+        acc_psum = ctx.enter_context(tc.psum_pool(name="acc", bufs=1))
+
+        x_chunks = {}
+
+        def load_x(s, c):
+            x_chunk = x_pool.tile([P, TILES, CHUNK], BF16)
+            nc.sync.dma_start(
+                out=x_chunk[:],
+                in_=streams[s].rearrange("b r d -> r b d")[:, :, c * CHUNK : (c + 1) * CHUNK],
+            )
+            x_chunks[(s, c)] = x_chunk
+
+        w_tiles = {}
+
+        def load_weights(s, h):
+            w_tile = w_pool.tile([P, W_GROUPS, 3 * E], U32, align_bytes=64)
+            for i, words in enumerate(words_of[s]):
+                nc.sync.dma_start(
+                    out=w_tile[:, :, i * E : (i + 1) * E].bitcast(I32),
+                    in_=words[h * W_GROUPS : (h + 1) * W_GROUPS]
+                    .rearrange("g p n t -> p g (n t)")
+                    .bitcast(I32),
+                )
+            w_tiles[(s, h)] = w_tile
+
+        w_planes = []
+
+        def load_scale_planes(s):
+            plane = const.tile([P, GROUPS, 3 * E], U8, align_bytes=64, name="w_plane%d" % s)
+            nc.vector.memset(plane[:].rearrange("p g n -> p (g n)").bitcast(I32), 0)
+            for i, scales in enumerate(scales_of[s]):
+                for quad in range(4):
+                    nc.sync.dma_start(
+                        out=plane[32 * quad : 32 * quad + 4, :, i * E : (i + 1) * E].bitcast(I32),
+                        in_=scales[:, 4 * quad : 4 * quad + 4, :]
+                        .rearrange("g r n -> r g n")
+                        .bitcast(I32),
+                    )
+            w_planes.append(plane)
+
+        gs_rows = const.tile([P, K_PASS], BF16)
+        for v, vector in enumerate((ln_t_g, ln_t_b, ln_i_g, ln_i_b)):
+            nc.gpsimd.dma_start(
+                out=gs_rows[v * GROUPS : (v + 1) * GROUPS, :],
+                in_=vector.rearrange("(g c) -> g c", c=K_PASS),
+            )
+        identity = const.tile([P, P], F32)
+        make_identity(nc, identity[:])
+
+        for c in range(CHUNKS):
+            load_x(0, c)
+        load_scale_planes(0)
+        for h in range(W_BUFS):
+            load_weights(0, h)
+        for c in range(X_BUFS - CHUNKS):
+            load_x(1, c)
+        load_scale_planes(1)
+        bias = const.tile([P, 5, E], BF16)
+        for slot, vector in enumerate((bq, bkt, bvt, bki, bvi)):
+            nc.sync.dma_start(out=bias[:, slot, :], in_=vector.partition_broadcast(P))
+        bias_slots = ((0, 1, 2), (0, 3, 4))
+
+        eps = const.tile([P, 1], F32)
+        nc.vector.memset(eps[:], EPS)
+        warm = const.tile([P, 1], F32)
+        nc.scalar.activation(out=warm[:], in_=eps[:], func=ACT.Sqrt)
+
+        gs_sorted = const.tile([P, PACK, P], F32)
+        nc.gpsimd.tensor_copy(out=gs_sorted[:], in_=gs_rows[:].rearrange("q (p t) -> q t p", t=PACK))
+        gs_bank = turn_psum.tile([P, PACK, P], F32, tag="bank")
+        for t in range(PACK):
+            nc.tensor.transpose(gs_bank[:, t, :], gs_sorted[:, t, :], identity[:])
+        gs_cols = const.tile([P, PACK, P], F32)
+
+        tuples = [const.tile([P, TILES, TUPLES, 3], F32, name="tuples%d" % s) for s in range(STREAMS)]
+        sums = [const.tile([P, TILES, len(SCALAR_CHUNKS)], F32, name="sums%d" % s) for s in range(STREAMS)]
+        neg_means = [const.tile([P, TILES, len(SCALAR_CHUNKS)], F32, name="neg_means%d" % s) for s in range(STREAMS)]
+        squares = [const.tile([P, TILES, len(SCALAR_CHUNKS)], F32, name="squares%d" % s) for s in range(STREAMS)]
+        mean_var = [const.tile([P, TILES, 2], F32, name="mean_var%d" % s) for s in range(STREAMS)]
+        std = [const.tile([P, TILES], F32, name="std%d" % s) for s in range(STREAMS)]
+        rstd = [const.tile([P, TILES], F32, name="rstd%d" % s) for s in range(STREAMS)]
+
+        def vector_stats(s, job):
+            e, rest = divmod(job, TILES * BLOCKS)
+            j, b = divmod(rest, BLOCKS)
+            first = 2 * (e * BLOCKS + b)
+            nc.vector.bn_stats(
+                out=tuples[s][:, j, first : first + 2, :].rearrange("p a b -> p (a b)"),
+                in_=x_chunks[(s, VECTOR_CHUNKS[e])][:, j, b * STAT_BLOCK : (b + 1) * STAT_BLOCK],
+            )
+
+        def scalar_stats(s, job):
+            e, rest = divmod(job, 2 * TILES)
+            second_pass, j = divmod(rest, TILES)
+            x_rows = x_chunks[(s, SCALAR_CHUNKS[e])][:, j, :]
+            unread = work.tile([P, CHUNK], BF16)
+            if second_pass:
+                nc.scalar.activation(
+                    out=unread[:], in_=x_rows, func=ACT.Square,
+                    bias=neg_means[s][:, j, e : e + 1], scale=1.0,
+                    accum_out=squares[s][:, j, e : e + 1],
+                )
+            else:
+                nc.scalar.activation(
+                    out=unread[:], in_=x_rows, func=ACT.Identity, accum_out=sums[s][:, j, e : e + 1]
+                )
+                nc.scalar.mul(out=neg_means[s][:, j, e : e + 1], in_=sums[s][:, j, e : e + 1], mul=-1.0 / CHUNK)
+
+        def aggregate(s):
+            nc.vector.memset(tuples[s][:, :, VECTOR_TUPLES:, 0], float(CHUNK))
+            nc.vector.tensor_scalar_mul(out=tuples[s][:, :, VECTOR_TUPLES:, 1], in0=sums[s][:], scalar1=1.0 / CHUNK)
+            nc.vector.tensor_copy(out=tuples[s][:, :, VECTOR_TUPLES:, 2], in_=squares[s][:])
+            for j in range(TILES):
+                nc.vector.bn_aggr(
+                    out=mean_var[s][:, j, :], in_=tuples[s][:, j, :, :].rearrange("p n c -> p (n c)")
+                )
+            nc.scalar.activation(out=std[s][:], in_=mean_var[s][:, :, 1], func=ACT.Sqrt, bias=eps[:, 0:1], scale=1.0)
+
+        def invert(s):
+            nc.vector.reciprocal(out=rstd[s][:], in_=std[s][:])
+
+        sorted_x = {}
+        banks = {}
+        planes_of = {}
+        grouped_of = {}
+        codes_of = {}
+        acc_of = {}
+
+        def normalise(r):
+            s, i = divmod(r, ROUNDS)
+            c, part = divmod(i, ROUNDS_PER_CHUNK)
+            xs = work.tile([P, TILES, ROUND_GROUPS, PACK, P], F32)
+            for j in range(TILES):
+                nc.vector.tensor_scalar(
+                    out=xs[:, j, :, :, :],
+                    in0=x_chunks[(s, c)][:, j, part * ROUND_COLS : (part + 1) * ROUND_COLS].rearrange(
+                        "r (g p t) -> r g t p", g=ROUND_GROUPS, t=PACK
+                    ),
+                    scalar1=mean_var[s][:, j, 0:1],
+                    scalar2=rstd[s][:, j : j + 1],
+                    op0=ALU.subtract,
+                    op1=ALU.mult,
+                )
+            sorted_x[r] = xs
+
+        def turn(r):
+            xs = sorted_x[r]
+            for gl in range(ROUND_GROUPS):
+                for half in range(PACK // 2):
+                    bank = turn_psum.tile([P, 2, ROWS], F32, tag="bank")
+                    for u in range(2):
+                        for j in range(TILES):
+                            nc.tensor.transpose(
+                                bank[:, u, j * P : (j + 1) * P], xs[:, j, gl, 2 * half + u, :], identity[:]
+                            )
+                    banks[(r, gl, half)] = bank
+
+        def gain_shift(r):
+            s, i = divmod(r, ROUNDS)
+            planes = work.tile([P, PACK, ROUND_GROUPS * ROWS], BF16)
+            for gl in range(ROUND_GROUPS):
+                g = i * ROUND_GROUPS + gl
+                for half in range(PACK // 2):
+                    for u in range(2):
+                        t = 2 * half + u
+                        nc.scalar.activation(
+                            out=planes[:, t, gl * ROWS : (gl + 1) * ROWS],
+                            in_=banks[(r, gl, half)][:, u, :],
+                            func=ACT.Identity,
+                            scale=gs_cols[:, t, 2 * s * GROUPS + g : 2 * s * GROUPS + g + 1],
+                            bias=gs_cols[:, t, (2 * s + 1) * GROUPS + g : (2 * s + 1) * GROUPS + g + 1],
+                        )
+            planes_of[r] = planes
+
+        def regroup(r):
+            grouped = work.tile([P, ROUND_GROUPS * ROWS, PACK], BF16, align_bytes=64)
+            nc.vector.tensor_copy(
+                out=grouped[:].rearrange("p (c i) t -> p c t i", i=4),
+                in_=planes_of[r][:].rearrange("p t (c i) -> p c t i", i=4),
+            )
+            grouped_of[r] = grouped
+
+        def quantise(r):
+            codes = mx_pool.tile([P, ROUND_GROUPS * ROWS], U32, align_bytes=64)
+            code_scales = mx_pool.tile([P, ROUND_GROUPS * ROWS], U8, align_bytes=64)
+            nc.vector.quantize_mx(
+                out=codes[:].bitcast(FP8X4),
+                scales=code_scales[:],
+                in_=grouped_of[r][:].rearrange("p c t -> p (c t)"),
+            )
+            codes_of[r] = (codes, code_scales)
+
+        def multiply(r):
+            s, i = divmod(r, ROUNDS)
+            if i == 0:
+                for j in range(TILES):
+                    acc_qk = acc_psum.tile([P, 2 * E], F32, name="acc_qk%d" % j)
+                    acc_v = acc_psum.tile([P, E], F32, name="acc_v%d" % j)
+                    acc_of[(s, j)] = (acc_qk, acc_v)
+            codes, code_scales = codes_of[r]
+            for gl in range(ROUND_GROUPS):
+                g = i * ROUND_GROUPS + gl
+                w_tile = w_tiles[(s, g // W_GROUPS)]
+                for j in range(TILES):
+                    tokens = slice(gl * ROWS + j * P, gl * ROWS + (j + 1) * P)
+                    for acc, cols in zip(acc_of[(s, j)], (slice(0, 2 * E), slice(2 * E, 3 * E))):
+                        nc.tensor.matmul_mx(
+                            out=acc[:],
+                            lhsT=codes[:, tokens].bitcast(FP8X4),
+                            lhsT_scale=code_scales[:, tokens],
+                            rhs=w_tile[:, g % W_GROUPS, cols].bitcast(FP8X4),
+                            rhs_scale=w_planes[s][:, g, cols],
+                            start=(g == 0),
+                            stop=(g == GROUPS - 1),
+                        )
+
+        def finish(s):
+            result = work.tile([P, TILES, 3 * E], F32)
+            for j in range(TILES):
+                acc_qk, acc_v = acc_of[(s, j)]
+                products = (acc_qk[:, 0:E], acc_qk[:, E : 2 * E], acc_v[:])
+                for i, product in enumerate(products):
+                    nc.vector.tensor_tensor(
+                        out=result[:, j, i * E : (i + 1) * E], in0=product,
+                        in1=bias[:, bias_slots[s][i], :], op=ALU.add,
+                    )
+            for i, out in enumerate(outs):
+                nc.sync.dma_start(
+                    out=out[TILES * s : TILES * (s + 1)].rearrange("b r n -> r b n"),
+                    in_=result[:, :, i * E : (i + 1) * E],
+                )
+
+        for job in range(SCALAR_JOBS):
+            scalar_stats(0, job)
+        for job in range(VECTOR_JOBS):
+            vector_stats(0, job)
+        aggregate(0)
+        nc.vector.tensor_copy(out=gs_cols[:], in_=gs_bank[:])
+        invert(0)
+
+        VECTOR_JOBS_A_ROUND = TILES * BLOCKS // ROUNDS_PER_CHUNK
+        STAT_ROUNDS = max(VECTOR_JOBS // VECTOR_JOBS_A_ROUND, SCALAR_JOBS)
+        for r in range(STREAMS * ROUNDS + 3):
+            if r < STREAMS * ROUNDS:
+                normalise(r)
+                turn(r)
+                gain_shift(r)
+            if 0 <= r - 1 < STREAMS * ROUNDS:
+                regroup(r - 1)
+            if 0 <= r - 2 < STREAMS * ROUNDS:
+                quantise(r - 2)
+            if 0 <= r - 3 < STREAMS * ROUNDS:
+                multiply(r - 3)
+                if (r - 3) % ROUNDS == ROUNDS - 1:
+                    finish((r - 3) // ROUNDS)
+                h = (r - 3) // ROUNDS_PER_W + W_BUFS
+                if (r - 3) % ROUNDS_PER_W == ROUNDS_PER_W - 1 and h < STREAMS * W_TILES:
+                    load_weights(h // W_TILES, h % W_TILES)
+            c = r // ROUNDS_PER_CHUNK + X_BUFS - CHUNKS
+            if r % ROUNDS_PER_CHUNK == ROUNDS_PER_CHUNK - 1 and c < CHUNKS:
+                load_x(1, c)
+            if r < STAT_ROUNDS:
+                for job in range(r * VECTOR_JOBS_A_ROUND, min((r + 1) * VECTOR_JOBS_A_ROUND, VECTOR_JOBS)):
+                    vector_stats(1, job)
+                if r < SCALAR_JOBS:
+                    scalar_stats(1, r)
+            if r == STAT_ROUNDS:
+                aggregate(1)
+                invert(1)

@@ -72,6 +72,7 @@ def tile_modalityadaptivemodule_pa_k_kernel(
         mx_pool = ctx.enter_context(tc.tile_pool(name="mx", bufs=3))
         turn_psum = ctx.enter_context(tc.psum_pool(name="turn", bufs=4))
         acc_psum = ctx.enter_context(tc.psum_pool(name="acc", bufs=1))
+        ctx.enter_context(tc.manual_schedule())
 
         x_chunks = {}
 
@@ -111,6 +112,11 @@ def tile_modalityadaptivemodule_pa_k_kernel(
                     )
             w_planes.append(plane)
 
+        eps = const.tile([P, 1], F32)
+        nc.vector.memset(eps[:], EPS)
+        warm = const.tile([P, 1], F32)
+        nc.scalar.activation(out=warm[:], in_=eps[:], func=ACT.Sqrt)
+
         gs_rows = const.tile([P, K_PASS], BF16)
         for v, vector in enumerate((ln_t_g, ln_t_b, ln_i_g, ln_i_b)):
             nc.gpsimd.dma_start(
@@ -132,11 +138,6 @@ def tile_modalityadaptivemodule_pa_k_kernel(
         for slot, vector in enumerate((bq, bkt, bvt, bki, bvi)):
             nc.sync.dma_start(out=bias[:, slot, :], in_=vector.partition_broadcast(P))
         bias_slots = ((0, 1, 2), (0, 3, 4))
-
-        eps = const.tile([P, 1], F32)
-        nc.vector.memset(eps[:], EPS)
-        warm = const.tile([P, 1], F32)
-        nc.scalar.activation(out=warm[:], in_=eps[:], func=ACT.Sqrt)
 
         gs_sorted = const.tile([P, PACK, P], F32)
         nc.gpsimd.tensor_copy(out=gs_sorted[:], in_=gs_rows[:].rearrange("q (p t) -> q t p", t=PACK))
@@ -230,7 +231,7 @@ def tile_modalityadaptivemodule_pa_k_kernel(
 
         def gain_shift(r):
             s, i = divmod(r, ROUNDS)
-            planes = work.tile([P, PACK, ROUND_GROUPS * ROWS], BF16)
+            planes = work.tile([P, PACK, ROUND_GROUPS * ROWS], BF16, bufs=3)
             for gl in range(ROUND_GROUPS):
                 g = i * ROUND_GROUPS + gl
                 for half in range(PACK // 2):
@@ -311,32 +312,32 @@ def tile_modalityadaptivemodule_pa_k_kernel(
         nc.vector.tensor_copy(out=gs_cols[:], in_=gs_bank[:])
         invert(0)
 
-        VECTOR_JOBS_A_ROUND = TILES * BLOCKS // ROUNDS_PER_CHUNK
-        STAT_ROUNDS = max(VECTOR_JOBS // VECTOR_JOBS_A_ROUND, SCALAR_JOBS)
-        for r in range(STREAMS * ROUNDS + 3):
-            if r < STREAMS * ROUNDS:
+        ALL_ROUNDS = STREAMS * ROUNDS
+        STAT_ROUNDS = SCALAR_JOBS
+        for r in range(ALL_ROUNDS + 5 + 1):
+            if r < ALL_ROUNDS:
                 normalise(r)
                 turn(r)
                 gain_shift(r)
-            if 0 <= r - 1 < STREAMS * ROUNDS:
-                regroup(r - 1)
-            if 0 <= r - 2 < STREAMS * ROUNDS:
-                quantise(r - 2)
-            if 0 <= r - 3 < STREAMS * ROUNDS:
-                multiply(r - 3)
-                if (r - 3) % ROUNDS == ROUNDS - 1:
-                    finish((r - 3) // ROUNDS)
-                h = (r - 3) // ROUNDS_PER_W + W_BUFS
-                if (r - 3) % ROUNDS_PER_W == ROUNDS_PER_W - 1 and h < STREAMS * W_TILES:
+            if 0 <= r - 2 < ALL_ROUNDS:
+                regroup(r - 2)
+            if 0 <= r - 3 < ALL_ROUNDS:
+                quantise(r - 3)
+            if r - 5 in (ROUNDS - 1, ALL_ROUNDS - 1):
+                finish((r - 5) // ROUNDS)
+            if 0 <= r - 4 < ALL_ROUNDS:
+                multiply(r - 4)
+                h = (r - 4) // ROUNDS_PER_W + W_BUFS
+                if (r - 4) % ROUNDS_PER_W == ROUNDS_PER_W - 1 and h < STREAMS * W_TILES:
                     load_weights(h // W_TILES, h % W_TILES)
             c = r // ROUNDS_PER_CHUNK + X_BUFS - CHUNKS
             if r % ROUNDS_PER_CHUNK == ROUNDS_PER_CHUNK - 1 and c < CHUNKS:
                 load_x(1, c)
             if r < STAT_ROUNDS:
-                for job in range(r * VECTOR_JOBS_A_ROUND, min((r + 1) * VECTOR_JOBS_A_ROUND, VECTOR_JOBS)):
+                for job in range(r * VECTOR_JOBS // STAT_ROUNDS, (r + 1) * VECTOR_JOBS // STAT_ROUNDS):
                     vector_stats(1, job)
-                if r < SCALAR_JOBS:
-                    scalar_stats(1, r)
+                scalar_stats(1, r)
             if r == STAT_ROUNDS:
                 aggregate(1)
+            if r == STAT_ROUNDS + 1:
                 invert(1)

@@ -154,6 +154,9 @@ def tile_modalityadaptivemodule_pa_k_kernel(
         std = [const.tile([P, TILES], F32, name="std%d" % s) for s in range(STREAMS)]
         rstd = [const.tile([P, TILES], F32, name="rstd%d" % s) for s in range(STREAMS)]
 
+        for s in range(STREAMS):
+            nc.vector.memset(tuples[s][:, :, VECTOR_TUPLES:, 0], float(CHUNK))
+
         def vector_stats(s, job):
             e, rest = divmod(job, TILES * BLOCKS)
             j, b = divmod(rest, BLOCKS)
@@ -178,10 +181,10 @@ def tile_modalityadaptivemodule_pa_k_kernel(
                 nc.scalar.activation(
                     out=unread[:], in_=x_rows, func=ACT.Identity, accum_out=sums[s][:, j, e : e + 1]
                 )
-                nc.scalar.mul(out=neg_means[s][:, j, e : e + 1], in_=sums[s][:, j, e : e + 1], mul=-1.0 / CHUNK)
+                if j == TILES - 1:
+                    nc.scalar.mul(out=neg_means[s][:, :, e], in_=sums[s][:, :, e], mul=-1.0 / CHUNK)
 
         def aggregate(s):
-            nc.vector.memset(tuples[s][:, :, VECTOR_TUPLES:, 0], float(CHUNK))
             nc.vector.tensor_scalar_mul(out=tuples[s][:, :, VECTOR_TUPLES:, 1], in0=sums[s][:], scalar1=1.0 / CHUNK)
             nc.vector.tensor_copy(out=tuples[s][:, :, VECTOR_TUPLES:, 2], in_=squares[s][:])
             for j in range(TILES):
@@ -200,32 +203,37 @@ def tile_modalityadaptivemodule_pa_k_kernel(
         codes_of = {}
         acc_of = {}
 
-        def normalise(r):
-            s, i = divmod(r, ROUNDS)
-            c, part = divmod(i, ROUNDS_PER_CHUNK)
-            xs = work.tile([P, TILES, ROUND_GROUPS, PACK, P], F32)
+        def normalise(s, c):
+            xs = work.tile([P, TILES, CHUNK // K_PASS, PACK, P], F32)
             for j in range(TILES):
                 nc.vector.tensor_scalar(
                     out=xs[:, j, :, :, :],
-                    in0=x_chunks[(s, c)][:, j, part * ROUND_COLS : (part + 1) * ROUND_COLS].rearrange(
-                        "r (g p t) -> r g t p", g=ROUND_GROUPS, t=PACK
-                    ),
+                    in0=x_chunks[(s, c)][:, j, :].rearrange("r (g p t) -> r g t p", p=P, t=PACK),
                     scalar1=mean_var[s][:, j, 0:1],
                     scalar2=rstd[s][:, j : j + 1],
                     op0=ALU.subtract,
                     op1=ALU.mult,
                 )
-            sorted_x[r] = xs
+            sorted_x[(s, c)] = xs
+
+        def next_chunk(s, c):
+            normalise(s, c)
+            if s == 0 and c + X_BUFS < STREAMS * CHUNKS:
+                load_x(1, c + X_BUFS - CHUNKS)
 
         def turn(r):
-            xs = sorted_x[r]
+            s, i = divmod(r, ROUNDS)
+            c, part = divmod(i, ROUNDS_PER_CHUNK)
+            xs = sorted_x[(s, c)]
             for gl in range(ROUND_GROUPS):
                 for half in range(PACK // 2):
                     bank = turn_psum.tile([P, 2, ROWS], F32, tag="bank")
                     for u in range(2):
                         for j in range(TILES):
                             nc.tensor.transpose(
-                                bank[:, u, j * P : (j + 1) * P], xs[:, j, gl, 2 * half + u, :], identity[:]
+                                bank[:, u, j * P : (j + 1) * P],
+                                xs[:, j, part * ROUND_GROUPS + gl, 2 * half + u, :],
+                                identity[:],
                             )
                     banks[(r, gl, half)] = bank
 
@@ -311,18 +319,20 @@ def tile_modalityadaptivemodule_pa_k_kernel(
         aggregate(0)
         nc.vector.tensor_copy(out=gs_cols[:], in_=gs_bank[:])
         invert(0)
+        next_chunk(0, 0)
 
         ALL_ROUNDS = STREAMS * ROUNDS
         STAT_ROUNDS = SCALAR_JOBS
         for r in range(ALL_ROUNDS + 5 + 1):
             if r < ALL_ROUNDS:
-                normalise(r)
                 turn(r)
                 gain_shift(r)
             if 0 <= r - 2 < ALL_ROUNDS:
                 regroup(r - 2)
             if 0 <= r - 3 < ALL_ROUNDS:
                 quantise(r - 3)
+            if (r + 1) % ROUNDS_PER_CHUNK == 0 and r + 1 < ALL_ROUNDS:
+                next_chunk(*divmod((r + 1) // ROUNDS_PER_CHUNK, CHUNKS))
             if r - 5 in (ROUNDS - 1, ALL_ROUNDS - 1):
                 finish((r - 5) // ROUNDS)
             if 0 <= r - 4 < ALL_ROUNDS:
@@ -330,9 +340,6 @@ def tile_modalityadaptivemodule_pa_k_kernel(
                 h = (r - 4) // ROUNDS_PER_W + W_BUFS
                 if (r - 4) % ROUNDS_PER_W == ROUNDS_PER_W - 1 and h < STREAMS * W_TILES:
                     load_weights(h // W_TILES, h % W_TILES)
-            c = r // ROUNDS_PER_CHUNK + X_BUFS - CHUNKS
-            if r % ROUNDS_PER_CHUNK == ROUNDS_PER_CHUNK - 1 and c < CHUNKS:
-                load_x(1, c)
             if r < STAT_ROUNDS:
                 for job in range(r * VECTOR_JOBS // STAT_ROUNDS, (r + 1) * VECTOR_JOBS // STAT_ROUNDS):
                     vector_stats(1, job)

@@ -74,6 +74,11 @@ def tile_modalityadaptivemodule_pa_k_kernel(
         acc_psum = ctx.enter_context(tc.psum_pool(name="acc", bufs=1))
         ctx.enter_context(tc.manual_schedule())
 
+        eps = const.tile([P, 1], F32)
+        nc.vector.memset(eps[:], EPS)
+        warm = const.tile([P, 1], F32)
+        nc.scalar.activation(out=warm[:], in_=eps[:], func=ACT.Sqrt)
+
         x_chunks = {}
 
         def load_x(s, c):
@@ -97,25 +102,26 @@ def tile_modalityadaptivemodule_pa_k_kernel(
                 )
             w_tiles[(s, h)] = w_tile
 
-        w_planes = []
+        w_planes = [const.tile([P, GROUPS, 3 * E], U8, align_bytes=64, name="w_plane%d" % s) for s in range(STREAMS)]
+        for s in range(STREAMS):
+            nc.vector.memset(w_planes[s][:].rearrange("p g n -> p (g n)").bitcast(I32), 0)
 
         def load_scale_planes(s):
-            plane = const.tile([P, GROUPS, 3 * E], U8, align_bytes=64, name="w_plane%d" % s)
-            nc.vector.memset(plane[:].rearrange("p g n -> p (g n)").bitcast(I32), 0)
             for i, scales in enumerate(scales_of[s]):
                 for quad in range(4):
                     nc.sync.dma_start(
-                        out=plane[32 * quad : 32 * quad + 4, :, i * E : (i + 1) * E].bitcast(I32),
+                        out=w_planes[s][32 * quad : 32 * quad + 4, :, i * E : (i + 1) * E].bitcast(I32),
                         in_=scales[:, 4 * quad : 4 * quad + 4, :]
                         .rearrange("g r n -> r g n")
                         .bitcast(I32),
                     )
-            w_planes.append(plane)
 
-        eps = const.tile([P, 1], F32)
-        nc.vector.memset(eps[:], EPS)
-        warm = const.tile([P, 1], F32)
-        nc.scalar.activation(out=warm[:], in_=eps[:], func=ACT.Sqrt)
+        bias = const.tile([P, 5, E], BF16)
+        bias_slots = ((0, 1, 2), (0, 3, 4))
+
+        def load_biases():
+            for slot, vector in enumerate((bq, bkt, bvt, bki, bvi)):
+                nc.sync.dma_start(out=bias[:, slot, :], in_=vector.partition_broadcast(P))
 
         gs_rows = const.tile([P, K_PASS], BF16)
         for v, vector in enumerate((ln_t_g, ln_t_b, ln_i_g, ln_i_b)):
@@ -128,16 +134,11 @@ def tile_modalityadaptivemodule_pa_k_kernel(
 
         for c in range(CHUNKS):
             load_x(0, c)
+        for c in range(X_BUFS - CHUNKS):
+            load_x(1, c)
         load_scale_planes(0)
         for h in range(W_BUFS):
             load_weights(0, h)
-        for c in range(X_BUFS - CHUNKS):
-            load_x(1, c)
-        load_scale_planes(1)
-        bias = const.tile([P, 5, E], BF16)
-        for slot, vector in enumerate((bq, bkt, bvt, bki, bvi)):
-            nc.sync.dma_start(out=bias[:, slot, :], in_=vector.partition_broadcast(P))
-        bias_slots = ((0, 1, 2), (0, 3, 4))
 
         gs_sorted = const.tile([P, PACK, P], F32)
         nc.gpsimd.tensor_copy(out=gs_sorted[:], in_=gs_rows[:].rearrange("q (p t) -> q t p", t=PACK))
@@ -346,5 +347,7 @@ def tile_modalityadaptivemodule_pa_k_kernel(
                 scalar_stats(1, r)
             if r == STAT_ROUNDS:
                 aggregate(1)
+                load_scale_planes(1)
+                load_biases()
             if r == STAT_ROUNDS + 1:
                 invert(1)

@@ -11,6 +11,7 @@ U8 = mybir.dt.uint8
 FP8X4 = mybir.dt.float8_e4m3fn_x4
 ACT = mybir.ActivationFunctionType
 ALU = mybir.AluOpType
+AXIS = mybir.AxisListType
 
 P = 128
 PACK = 4
@@ -27,19 +28,29 @@ CHUNK = 2048
 CHUNKS = D // CHUNK
 X_BUFS = 12
 STAT_BLOCK = 512
-BLOCKS = CHUNK // STAT_BLOCK
 
-SCALAR_CHUNKS = [c for c in range(CHUNKS) if c % 3 == 0]
-VECTOR_CHUNKS = [c for c in range(CHUNKS) if c % 3 != 0]
-VECTOR_TUPLES = 2 * BLOCKS * len(VECTOR_CHUNKS)
-TUPLES = VECTOR_TUPLES + len(SCALAR_CHUNKS)
-VECTOR_JOBS = TILES * BLOCKS * len(VECTOR_CHUNKS)
-SCALAR_JOBS = 2 * TILES * len(SCALAR_CHUNKS)
+UNIT = CHUNK // 2
+UNITS = D // UNIT
+SCALAR_UNITS = [u for u in range(UNITS - 2) if u % 2 == 1] + [UNITS - 2]
+VECTOR_UNITS = [u for u in range(UNITS - 2) if u % 2 == 0] + [UNITS - 1]
+UNIT_BLOCKS = UNIT // STAT_BLOCK
+STEPS = len(VECTOR_UNITS)
+SCALAR_UNITS_IMG = [1, 3, 5, 7, 9, 11]
+VECTOR_UNITS_IMG = [u for u in range(UNITS) if u not in SCALAR_UNITS_IMG]
+UNITS_OF = ((VECTOR_UNITS, SCALAR_UNITS), (VECTOR_UNITS_IMG, SCALAR_UNITS_IMG))
+SCALAR_COLS = [UNIT * len(scalar_units) for vector_units, scalar_units in UNITS_OF]
+TUPLES = [2 * UNIT_BLOCKS * len(vector_units) for vector_units, scalar_units in UNITS_OF]
+VECTOR_JOBS = [TILES * UNIT_BLOCKS * len(vector_units) for vector_units, scalar_units in UNITS_OF]
+SCALAR_JOBS = 2 * TILES * len(SCALAR_UNITS_IMG)
+HEAD_JOBS = 4
+HEAD_VECTOR = 2
 
 ROUND_GROUPS = 2
 ROUND_COLS = ROUND_GROUPS * K_PASS
 ROUNDS = GROUPS // ROUND_GROUPS
 ROUNDS_PER_CHUNK = CHUNK // ROUND_COLS
+CHUNK_GROUPS = CHUNK // K_PASS
+VECTOR_SLOTS = (PACK, PACK - 1)
 W_GROUPS = 4
 W_TILES = GROUPS // W_GROUPS
 W_BUFS = 4
@@ -81,12 +92,14 @@ def tile_modalityadaptivemodule_pa_k_kernel(
 
         x_chunks = {}
 
-        def load_x(s, c):
+        def load_x(s, c, pieces=1):
             x_chunk = x_pool.tile([P, TILES, CHUNK], BF16)
-            nc.sync.dma_start(
-                out=x_chunk[:],
-                in_=streams[s].rearrange("b r d -> r b d")[:, :, c * CHUNK : (c + 1) * CHUNK],
-            )
+            width = CHUNK // pieces
+            for i in range(pieces):
+                nc.sync.dma_start(
+                    out=x_chunk[:, :, i * width : (i + 1) * width],
+                    in_=streams[s].rearrange("b r d -> r b d")[:, :, c * CHUNK + i * width : c * CHUNK + (i + 1) * width],
+                )
             x_chunks[(s, c)] = x_chunk
 
         w_tiles = {}
@@ -103,8 +116,6 @@ def tile_modalityadaptivemodule_pa_k_kernel(
             w_tiles[(s, h)] = w_tile
 
         w_planes = [const.tile([P, GROUPS, 3 * E], U8, align_bytes=64, name="w_plane%d" % s) for s in range(STREAMS)]
-        for s in range(STREAMS):
-            nc.vector.memset(w_planes[s][:].rearrange("p g n -> p (g n)").bitcast(I32), 0)
 
         def load_scale_planes(s):
             for i, scales in enumerate(scales_of[s]):
@@ -131,9 +142,13 @@ def tile_modalityadaptivemodule_pa_k_kernel(
             )
         identity = const.tile([P, P], F32)
         make_identity(nc, identity[:])
+        identity_bf = const.tile([P, P], BF16)
+        nc.gpsimd.tensor_copy(out=identity_bf[:], in_=identity[:])
+        for s in range(STREAMS):
+            nc.gpsimd.memset(w_planes[s][:].rearrange("p g n -> p (g n)").bitcast(I32), 0)
 
         for c in range(CHUNKS):
-            load_x(0, c)
+            load_x(0, c, pieces=2 if c in (0, CHUNKS - 1) else 1)
         for c in range(X_BUFS - CHUNKS):
             load_x(1, c)
         load_scale_planes(0)
@@ -142,60 +157,99 @@ def tile_modalityadaptivemodule_pa_k_kernel(
 
         gs_sorted = const.tile([P, PACK, P], F32)
         nc.gpsimd.tensor_copy(out=gs_sorted[:], in_=gs_rows[:].rearrange("q (p t) -> q t p", t=PACK))
-        gs_bank = turn_psum.tile([P, PACK, P], F32, tag="bank")
-        for t in range(PACK):
-            nc.tensor.transpose(gs_bank[:, t, :], gs_sorted[:, t, :], identity[:])
         gs_cols = const.tile([P, PACK, P], F32)
 
-        tuples = [const.tile([P, TILES, TUPLES, 3], F32, name="tuples%d" % s) for s in range(STREAMS)]
-        sums = [const.tile([P, TILES, len(SCALAR_CHUNKS)], F32, name="sums%d" % s) for s in range(STREAMS)]
-        neg_means = [const.tile([P, TILES, len(SCALAR_CHUNKS)], F32, name="neg_means%d" % s) for s in range(STREAMS)]
-        squares = [const.tile([P, TILES, len(SCALAR_CHUNKS)], F32, name="squares%d" % s) for s in range(STREAMS)]
+        tuples = [const.tile([P, TILES, TUPLES[s] + 1, 3], F32, name="tuples%d" % s) for s in range(STREAMS)]
+        squares = [const.tile([P, TILES, len(UNITS_OF[s][1])], F32, name="squares%d" % s) for s in range(STREAMS)]
+        sums = [const.tile([P, TILES, len(UNITS_OF[s][1])], F32, name="sums%d" % s) for s in range(STREAMS)]
+        total = [const.tile([P, TILES], F32, name="total%d" % s) for s in range(STREAMS)]
+        offset = [const.tile([P, TILES], F32, name="offset%d" % s) for s in range(STREAMS)]
+        excess = [const.tile([P, TILES], F32, name="excess%d" % s) for s in range(STREAMS)]
+        square_sum = [const.tile([P, TILES], F32, name="square_sum%d" % s) for s in range(STREAMS)]
         mean_var = [const.tile([P, TILES, 2], F32, name="mean_var%d" % s) for s in range(STREAMS)]
         std = [const.tile([P, TILES], F32, name="std%d" % s) for s in range(STREAMS)]
         rstd = [const.tile([P, TILES], F32, name="rstd%d" % s) for s in range(STREAMS)]
+        lift = const.tile([P, TILES], F32)
+        sum_banks = [turn_psum.tile([P, STAT_BLOCK], F32, tag="bank", name="sum_bank%d" % j) for j in range(TILES)]
 
         for s in range(STREAMS):
-            nc.vector.memset(tuples[s][:, :, VECTOR_TUPLES:, 0], float(CHUNK))
+            nc.vector.memset(tuples[s][:, :, TUPLES[s], 0], float(SCALAR_COLS[s]))
+
+        def unit_rows(s, unit, j):
+            c, half = divmod(unit, 2)
+            return x_chunks[(s, c)][:, j, half * UNIT : (half + 1) * UNIT]
 
         def vector_stats(s, job):
-            e, rest = divmod(job, TILES * BLOCKS)
-            j, b = divmod(rest, BLOCKS)
-            first = 2 * (e * BLOCKS + b)
+            block, j = divmod(job, TILES)
+            step, b = divmod(block, UNIT_BLOCKS)
             nc.vector.bn_stats(
-                out=tuples[s][:, j, first : first + 2, :].rearrange("p a b -> p (a b)"),
-                in_=x_chunks[(s, VECTOR_CHUNKS[e])][:, j, b * STAT_BLOCK : (b + 1) * STAT_BLOCK],
+                out=tuples[s][:, j, 2 * block : 2 * block + 2, :].rearrange("p a b -> p (a b)"),
+                in_=unit_rows(s, UNITS_OF[s][0][step], j)[:, b * STAT_BLOCK : (b + 1) * STAT_BLOCK],
             )
 
-        def scalar_stats(s, job):
-            e, rest = divmod(job, 2 * TILES)
-            second_pass, j = divmod(rest, TILES)
-            x_rows = x_chunks[(s, SCALAR_CHUNKS[e])][:, j, :]
-            unread = work.tile([P, CHUNK], BF16)
-            if second_pass:
-                nc.scalar.activation(
-                    out=unread[:], in_=x_rows, func=ACT.Square,
-                    bias=neg_means[s][:, j, e : e + 1], scale=1.0,
-                    accum_out=squares[s][:, j, e : e + 1],
+        def square(s, step, j):
+            unread = work.tile([P, UNIT], BF16)
+            nc.scalar.activation(
+                out=unread[:], in_=unit_rows(s, UNITS_OF[s][1][step], j), func=ACT.Square,
+                bias=tuples[s][:, j, 0, 1:2], scale=-1.0, accum_out=squares[s][:, j, step : step + 1],
+            )
+
+        def add_up(s, step, j):
+            unread = work.tile([P, UNIT], BF16)
+            nc.scalar.activation(
+                out=unread[:], in_=unit_rows(s, UNITS_OF[s][1][step], j), func=ACT.Identity,
+                accum_out=sums[s][:, j, step : step + 1],
+            )
+
+        def add_up_text(step, j):
+            for b in range(UNIT_BLOCKS):
+                nc.tensor.matmul(
+                    sum_banks[j][:], lhsT=identity_bf[:],
+                    rhs=unit_rows(0, SCALAR_UNITS[step], j)[:, b * STAT_BLOCK : (b + 1) * STAT_BLOCK],
+                    start=(step == 0 and b == 0), stop=(step == STEPS - 1 and b == UNIT_BLOCKS - 1),
                 )
-            else:
-                nc.scalar.activation(
-                    out=unread[:], in_=x_rows, func=ACT.Identity, accum_out=sums[s][:, j, e : e + 1]
-                )
-                if j == TILES - 1:
-                    nc.scalar.mul(out=neg_means[s][:, :, e], in_=sums[s][:, :, e], mul=-1.0 / CHUNK)
+
+        def scalar_stats_img(job):
+            step, rest = divmod(job, 2 * TILES)
+            second, j = divmod(rest, TILES)
+            (add_up if second else square)(1, step, j)
+
+        def total_text():
+            for j in range(TILES):
+                nc.vector.tensor_reduce(out=total[0][:, j : j + 1], in_=sum_banks[j][:], axis=AXIS.X, op=ALU.add)
+
+        def total_img():
+            nc.vector.tensor_reduce(out=total[1][:], in_=sums[1][:], axis=AXIS.X, op=ALU.add)
+
+        def scalar_mean(s):
+            nc.vector.tensor_scalar_mul(out=tuples[s][:, :, TUPLES[s], 1], in0=total[s][:], scalar1=1.0 / SCALAR_COLS[s])
+
+        def mean_offset(s):
+            nc.vector.tensor_tensor(out=offset[s][:], in0=tuples[s][:, :, TUPLES[s], 1], in1=tuples[s][:, :, 0, 1], op=ALU.subtract)
+
+        def offset_excess(s):
+            nc.vector.scalar_tensor_tensor(
+                out=excess[s][:], in0=offset[s][:], scalar=float(SCALAR_COLS[s]), in1=offset[s][:], op0=ALU.mult, op1=ALU.mult
+            )
+
+        def total_square(s):
+            nc.vector.tensor_reduce(out=square_sum[s][:], in_=squares[s][:], axis=AXIS.X, op=ALU.add)
+
+        def scalar_m2(s):
+            nc.vector.tensor_tensor(out=tuples[s][:, :, TUPLES[s], 2], in0=square_sum[s][:], in1=excess[s][:], op=ALU.subtract)
 
         def aggregate(s):
-            nc.vector.tensor_scalar_mul(out=tuples[s][:, :, VECTOR_TUPLES:, 1], in0=sums[s][:], scalar1=1.0 / CHUNK)
-            nc.vector.tensor_copy(out=tuples[s][:, :, VECTOR_TUPLES:, 2], in_=squares[s][:])
             for j in range(TILES):
-                nc.vector.bn_aggr(
-                    out=mean_var[s][:, j, :], in_=tuples[s][:, j, :, :].rearrange("p n c -> p (n c)")
-                )
+                nc.vector.bn_aggr(out=mean_var[s][:, j, :], in_=tuples[s][:, j, :, :].rearrange("p n c -> p (n c)"))
             nc.scalar.activation(out=std[s][:], in_=mean_var[s][:, :, 1], func=ACT.Sqrt, bias=eps[:, 0:1], scale=1.0)
 
         def invert(s):
             nc.vector.reciprocal(out=rstd[s][:], in_=std[s][:])
+
+        def lift_img():
+            nc.vector.scalar_tensor_tensor(
+                out=lift[:], in0=mean_var[1][:, :, 0], scalar=-1.0, in1=rstd[1][:], op0=ALU.mult, op1=ALU.mult
+            )
 
         sorted_x = {}
         banks = {}
@@ -205,16 +259,23 @@ def tile_modalityadaptivemodule_pa_k_kernel(
         acc_of = {}
 
         def normalise(s, c):
-            xs = work.tile([P, TILES, CHUNK // K_PASS, PACK, P], F32)
+            xs = work.tile([P, TILES, CHUNK_GROUPS, PACK, P], F32)
             for j in range(TILES):
+                cut = VECTOR_SLOTS[s] if j == TILES - 1 else PACK
+                x_sorted = x_chunks[(s, c)][:, j, :].rearrange("r (g p t) -> r g t p", p=P, t=PACK)
                 nc.vector.tensor_scalar(
-                    out=xs[:, j, :, :, :],
-                    in0=x_chunks[(s, c)][:, j, :].rearrange("r (g p t) -> r g t p", p=P, t=PACK),
+                    out=xs[:, j, :, 0:cut, :],
+                    in0=x_sorted[:, :, 0:cut],
                     scalar1=mean_var[s][:, j, 0:1],
                     scalar2=rstd[s][:, j : j + 1],
                     op0=ALU.subtract,
                     op1=ALU.mult,
                 )
+                for u in range(cut, PACK):
+                    nc.scalar.activation(
+                        out=xs[:, j, :, u, :], in_=x_sorted[:, :, u], func=ACT.Identity,
+                        scale=rstd[s][:, j : j + 1], bias=lift[:, j : j + 1],
+                    )
             sorted_x[(s, c)] = xs
 
         def next_chunk(s, c):
@@ -313,25 +374,66 @@ def tile_modalityadaptivemodule_pa_k_kernel(
                     in_=result[:, :, i * E : (i + 1) * E],
                 )
 
-        for job in range(SCALAR_JOBS):
-            scalar_stats(0, job)
-        for job in range(VECTOR_JOBS):
+        STEP_JOBS = VECTOR_JOBS[0] // STEPS
+        for step in range(STEPS):
+            last = step == STEPS - 1
+            if not last:
+                for job in range(step * STEP_JOBS, (step + 1) * STEP_JOBS):
+                    vector_stats(0, job)
+            for j in range(TILES):
+                square(0, step, j)
+                add_up_text(step, j)
+        total_text()
+        scalar_mean(0)
+        mean_offset(0)
+        offset_excess(0)
+        for job in range(VECTOR_JOBS[0] - STEP_JOBS, VECTOR_JOBS[0]):
             vector_stats(0, job)
+        gs_bank = turn_psum.tile([P, PACK, P], F32, tag="bank")
+        for t in range(PACK):
+            nc.tensor.transpose(gs_bank[:, t, :], gs_sorted[:, t, :], identity[:])
+        total_square(0)
+        for job in range(HEAD_VECTOR):
+            vector_stats(1, job)
+        scalar_m2(0)
         aggregate(0)
+        for job in range(HEAD_JOBS):
+            scalar_stats_img(job)
         nc.vector.tensor_copy(out=gs_cols[:], in_=gs_bank[:])
         invert(0)
         next_chunk(0, 0)
 
         ALL_ROUNDS = STREAMS * ROUNDS
-        STAT_ROUNDS = SCALAR_JOBS
+        STAT_ROUNDS = 12
+
+        def first_vector(r):
+            return HEAD_VECTOR + r * (VECTOR_JOBS[1] - HEAD_VECTOR) // STAT_ROUNDS
+
+        def first_scalar(r):
+            return HEAD_JOBS + r * (SCALAR_JOBS - HEAD_JOBS) // STAT_ROUNDS
+
+        img_steps = {
+            STAT_ROUNDS: (total_img, lambda: scalar_mean(1), lambda: mean_offset(1)),
+            STAT_ROUNDS + 1: (lambda: offset_excess(1), lambda: total_square(1), lambda: scalar_m2(1)),
+            STAT_ROUNDS + 2: (lambda: aggregate(1),),
+            STAT_ROUNDS + 3: (lambda: invert(1), lift_img),
+        }
+
+        def img_step(r, i):
+            steps = img_steps.get(r, ())
+            if i < len(steps):
+                steps[i]()
+
         for r in range(ALL_ROUNDS + 5 + 1):
             if r < ALL_ROUNDS:
                 turn(r)
                 gain_shift(r)
             if 0 <= r - 2 < ALL_ROUNDS:
                 regroup(r - 2)
+            img_step(r, 0)
             if 0 <= r - 3 < ALL_ROUNDS:
                 quantise(r - 3)
+            img_step(r, 1)
             if (r + 1) % ROUNDS_PER_CHUNK == 0 and r + 1 < ALL_ROUNDS:
                 next_chunk(*divmod((r + 1) // ROUNDS_PER_CHUNK, CHUNKS))
             if r - 5 in (ROUNDS - 1, ALL_ROUNDS - 1):
@@ -342,12 +444,11 @@ def tile_modalityadaptivemodule_pa_k_kernel(
                 if (r - 4) % ROUNDS_PER_W == ROUNDS_PER_W - 1 and h < STREAMS * W_TILES:
                     load_weights(h // W_TILES, h % W_TILES)
             if r < STAT_ROUNDS:
-                for job in range(r * VECTOR_JOBS // STAT_ROUNDS, (r + 1) * VECTOR_JOBS // STAT_ROUNDS):
+                for job in range(first_vector(r), first_vector(r + 1)):
                     vector_stats(1, job)
-                scalar_stats(1, r)
-            if r == STAT_ROUNDS:
-                aggregate(1)
+                for job in range(first_scalar(r), first_scalar(r + 1)):
+                    scalar_stats_img(job)
+            if r == STAT_ROUNDS - 1:
                 load_scale_planes(1)
                 load_biases()
-            if r == STAT_ROUNDS + 1:
-                invert(1)
+            img_step(r, 2)

@@ -31,19 +31,25 @@ STAT_BLOCK = 512
 
 UNIT = CHUNK // 2
 UNITS = D // UNIT
-SCALAR_UNITS = [u for u in range(UNITS - 2) if u % 2 == 1] + [UNITS - 2]
-VECTOR_UNITS = [u for u in range(UNITS - 2) if u % 2 == 0] + [UNITS - 1]
+SCALAR_UNITS = [u for u in range(UNITS - 2) if u % 2 == 1]
+VECTOR_UNITS = [u for u in range(UNITS) if u not in SCALAR_UNITS]
 UNIT_BLOCKS = UNIT // STAT_BLOCK
-STEPS = len(VECTOR_UNITS)
+STEPS = len(SCALAR_UNITS)
 SCALAR_UNITS_IMG = [1, 3, 5, 7, 9, 11]
+TENSOR_STEPS_IMG = 2
 VECTOR_UNITS_IMG = [u for u in range(UNITS) if u not in SCALAR_UNITS_IMG]
 UNITS_OF = ((VECTOR_UNITS, SCALAR_UNITS), (VECTOR_UNITS_IMG, SCALAR_UNITS_IMG))
 SCALAR_COLS = [UNIT * len(scalar_units) for vector_units, scalar_units in UNITS_OF]
 TUPLES = [2 * UNIT_BLOCKS * len(vector_units) for vector_units, scalar_units in UNITS_OF]
 VECTOR_JOBS = [TILES * UNIT_BLOCKS * len(vector_units) for vector_units, scalar_units in UNITS_OF]
-SCALAR_JOBS = 2 * TILES * len(SCALAR_UNITS_IMG)
+SCALAR_JOBS = [
+    (square, step, j)
+    for step in range(len(SCALAR_UNITS_IMG))
+    for square in ((True,) if step < TENSOR_STEPS_IMG else (False, True))
+    for j in range(TILES)
+]
 HEAD_JOBS = 4
-HEAD_VECTOR = 2
+HEAD_VECTOR = 4
 
 ROUND_GROUPS = 2
 ROUND_COLS = ROUND_GROUPS * K_PASS
@@ -116,6 +122,7 @@ def tile_modalityadaptivemodule_pa_k_kernel(
             w_tiles[(s, h)] = w_tile
 
         w_planes = [const.tile([P, GROUPS, 3 * E], U8, align_bytes=64, name="w_plane%d" % s) for s in range(STREAMS)]
+        nc.vector.memset(w_planes[0][:].rearrange("p g n -> p (g n)").bitcast(I32), 0)
 
         def load_scale_planes(s):
             for i, scales in enumerate(scales_of[s]):
@@ -144,11 +151,10 @@ def tile_modalityadaptivemodule_pa_k_kernel(
         make_identity(nc, identity[:])
         identity_bf = const.tile([P, P], BF16)
         nc.gpsimd.tensor_copy(out=identity_bf[:], in_=identity[:])
-        for s in range(STREAMS):
-            nc.gpsimd.memset(w_planes[s][:].rearrange("p g n -> p (g n)").bitcast(I32), 0)
+        nc.gpsimd.memset(w_planes[1][:].rearrange("p g n -> p (g n)").bitcast(I32), 0)
 
         for c in range(CHUNKS):
-            load_x(0, c, pieces=2 if c in (0, CHUNKS - 1) else 1)
+            load_x(0, c, pieces=4 if c == 0 else 2)
         for c in range(X_BUFS - CHUNKS):
             load_x(1, c)
         load_scale_planes(0)
@@ -161,8 +167,7 @@ def tile_modalityadaptivemodule_pa_k_kernel(
 
         tuples = [const.tile([P, TILES, TUPLES[s] + 1, 3], F32, name="tuples%d" % s) for s in range(STREAMS)]
         squares = [const.tile([P, TILES, len(UNITS_OF[s][1])], F32, name="squares%d" % s) for s in range(STREAMS)]
-        sums = [const.tile([P, TILES, len(UNITS_OF[s][1])], F32, name="sums%d" % s) for s in range(STREAMS)]
-        total = [const.tile([P, TILES], F32, name="total%d" % s) for s in range(STREAMS)]
+        sums = const.tile([P, TILES, len(SCALAR_UNITS_IMG)], F32)
         offset = [const.tile([P, TILES], F32, name="offset%d" % s) for s in range(STREAMS)]
         excess = [const.tile([P, TILES], F32, name="excess%d" % s) for s in range(STREAMS)]
         square_sum = [const.tile([P, TILES], F32, name="square_sum%d" % s) for s in range(STREAMS)]
@@ -170,7 +175,6 @@ def tile_modalityadaptivemodule_pa_k_kernel(
         std = [const.tile([P, TILES], F32, name="std%d" % s) for s in range(STREAMS)]
         rstd = [const.tile([P, TILES], F32, name="rstd%d" % s) for s in range(STREAMS)]
         lift = const.tile([P, TILES], F32)
-        sum_banks = [turn_psum.tile([P, STAT_BLOCK], F32, tag="bank", name="sum_bank%d" % j) for j in range(TILES)]
 
         for s in range(STREAMS):
             nc.vector.memset(tuples[s][:, :, TUPLES[s], 0], float(SCALAR_COLS[s]))
@@ -198,31 +202,40 @@ def tile_modalityadaptivemodule_pa_k_kernel(
             unread = work.tile([P, UNIT], BF16)
             nc.scalar.activation(
                 out=unread[:], in_=unit_rows(s, UNITS_OF[s][1][step], j), func=ACT.Identity,
-                accum_out=sums[s][:, j, step : step + 1],
+                scale=1.0 / SCALAR_COLS[s], accum_out=sums[:, j, step : step + 1],
             )
 
-        def add_up_text(step, j):
-            for b in range(UNIT_BLOCKS):
+        def add_up_on_tensor(s, step, j, steps):
+            for b in range(UNIT // P):
                 nc.tensor.matmul(
-                    sum_banks[j][:], lhsT=identity_bf[:],
-                    rhs=unit_rows(0, SCALAR_UNITS[step], j)[:, b * STAT_BLOCK : (b + 1) * STAT_BLOCK],
-                    start=(step == 0 and b == 0), stop=(step == STEPS - 1 and b == UNIT_BLOCKS - 1),
+                    sum_banks[(s, j)][:], lhsT=identity_bf[:],
+                    rhs=unit_rows(s, UNITS_OF[s][1][step], j)[:, b * P : (b + 1) * P],
+                    start=(step == 0 and b == 0), stop=(step == steps - 1 and b == UNIT // P - 1),
                 )
 
-        def scalar_stats_img(job):
-            step, rest = divmod(job, 2 * TILES)
-            second, j = divmod(rest, TILES)
-            (add_up if second else square)(1, step, j)
-
-        def total_text():
+        def add_up_bank(s, out):
             for j in range(TILES):
-                nc.vector.tensor_reduce(out=total[0][:, j : j + 1], in_=sum_banks[j][:], axis=AXIS.X, op=ALU.add)
+                unread = work.tile([P, UNIT], BF16)
+                nc.scalar.activation(
+                    out=unread[:, 0:P], in_=sum_banks[(s, j)][:], func=ACT.Identity, scale=1.0 / SCALAR_COLS[s],
+                    accum_out=out[:, j, :],
+                )
 
-        def total_img():
-            nc.vector.tensor_reduce(out=total[1][:], in_=sums[1][:], axis=AXIS.X, op=ALU.add)
+        sum_banks = {}
 
-        def scalar_mean(s):
-            nc.vector.tensor_scalar_mul(out=tuples[s][:, :, TUPLES[s], 1], in0=total[s][:], scalar1=1.0 / SCALAR_COLS[s])
+        def open_sums(s):
+            for j in range(TILES):
+                sum_bank = turn_psum.tile([P, P], F32, tag="bank")
+                sum_banks[(s, j)] = sum_bank
+
+        def scalar_stats_img(job):
+            squared, step, j = SCALAR_JOBS[job]
+            (square if squared else add_up)(1, step, j)
+
+        def mean_img():
+            nc.vector.tensor_reduce(
+                out=tuples[1][:, :, TUPLES[1], 1], in_=sums[:, :, TENSOR_STEPS_IMG - 1 :], axis=AXIS.X, op=ALU.add
+            )
 
         def mean_offset(s):
             nc.vector.tensor_tensor(out=offset[s][:], in0=tuples[s][:, :, TUPLES[s], 1], in1=tuples[s][:, :, 0, 1], op=ALU.subtract)
@@ -258,14 +271,16 @@ def tile_modalityadaptivemodule_pa_k_kernel(
         codes_of = {}
         acc_of = {}
 
-        def normalise(s, c):
+        def normalise(s, c, parts=1):
             xs = work.tile([P, TILES, CHUNK_GROUPS, PACK, P], F32)
-            for j in range(TILES):
+            sorted_x[(s, c)] = xs
+            for part, j in [(part, j) for part in range(parts) for j in range(TILES)]:
                 cut = VECTOR_SLOTS[s] if j == TILES - 1 else PACK
+                gs = slice(part * CHUNK_GROUPS // parts, (part + 1) * CHUNK_GROUPS // parts)
                 x_sorted = x_chunks[(s, c)][:, j, :].rearrange("r (g p t) -> r g t p", p=P, t=PACK)
                 nc.vector.tensor_scalar(
-                    out=xs[:, j, :, 0:cut, :],
-                    in0=x_sorted[:, :, 0:cut],
+                    out=xs[:, j, gs, 0:cut, :],
+                    in0=x_sorted[:, gs, 0:cut],
                     scalar1=mean_var[s][:, j, 0:1],
                     scalar2=rstd[s][:, j : j + 1],
                     op0=ALU.subtract,
@@ -273,13 +288,12 @@ def tile_modalityadaptivemodule_pa_k_kernel(
                 )
                 for u in range(cut, PACK):
                     nc.scalar.activation(
-                        out=xs[:, j, :, u, :], in_=x_sorted[:, :, u], func=ACT.Identity,
+                        out=xs[:, j, gs, u, :], in_=x_sorted[:, gs, u], func=ACT.Identity,
                         scale=rstd[s][:, j : j + 1], bias=lift[:, j : j + 1],
                     )
-            sorted_x[(s, c)] = xs
 
         def next_chunk(s, c):
-            normalise(s, c)
+            normalise(s, c, parts=2 if (s, c) == (0, 0) else 1)
             if s == 0 and c + X_BUFS < STREAMS * CHUNKS:
                 load_x(1, c + X_BUFS - CHUNKS)
 
@@ -374,33 +388,41 @@ def tile_modalityadaptivemodule_pa_k_kernel(
                     in_=result[:, :, i * E : (i + 1) * E],
                 )
 
-        STEP_JOBS = VECTOR_JOBS[0] // STEPS
-        for step in range(STEPS):
-            last = step == STEPS - 1
-            if not last:
-                for job in range(step * STEP_JOBS, (step + 1) * STEP_JOBS):
-                    vector_stats(0, job)
-            for j in range(TILES):
-                square(0, step, j)
-                add_up_text(step, j)
-        total_text()
-        scalar_mean(0)
-        mean_offset(0)
-        offset_excess(0)
-        for job in range(VECTOR_JOBS[0] - STEP_JOBS, VECTOR_JOBS[0]):
-            vector_stats(0, job)
         gs_bank = turn_psum.tile([P, PACK, P], F32, tag="bank")
         for t in range(PACK):
             nc.tensor.transpose(gs_bank[:, t, :], gs_sorted[:, t, :], identity[:])
-        total_square(0)
-        for job in range(HEAD_VECTOR):
-            vector_stats(1, job)
-        scalar_m2(0)
-        aggregate(0)
-        for job in range(HEAD_JOBS):
+        UNIT_JOBS = TILES * UNIT_BLOCKS
+        open_sums(0)
+        for step in range(STEPS):
+            for job in range(step * UNIT_JOBS, (step + 1) * UNIT_JOBS):
+                vector_stats(0, job)
+            if step == 1:
+                nc.vector.tensor_copy(out=gs_cols[:], in_=gs_bank[:])
+            for j in range(TILES):
+                square(0, step, j)
+                add_up_on_tensor(0, step, j, STEPS)
+        add_up_bank(0, tuples[0][:, :, TUPLES[0], 1:2])
+        open_sums(1)
+        for step in range(TENSOR_STEPS_IMG):
+            for j in range(TILES):
+                add_up_on_tensor(1, step, j, TENSOR_STEPS_IMG)
+        text_steps = [total_square, mean_offset, offset_excess, scalar_m2]
+        for job in range(STEPS * UNIT_JOBS, VECTOR_JOBS[0]):
+            vector_stats(0, job)
+            if job == VECTOR_JOBS[0] - 2 - len(text_steps):
+                for img_job in range(HEAD_VECTOR // 2):
+                    vector_stats(1, img_job)
+            if job > VECTOR_JOBS[0] - 2 - len(text_steps) and text_steps:
+                text_steps.pop(0)(0)
+        for job in range(HEAD_JOBS // 2):
             scalar_stats_img(job)
-        nc.vector.tensor_copy(out=gs_cols[:], in_=gs_bank[:])
+        aggregate(0)
+        for job in range(HEAD_VECTOR // 2, HEAD_VECTOR):
+            vector_stats(1, job)
         invert(0)
+        add_up_bank(1, sums[:, :, TENSOR_STEPS_IMG - 1 : TENSOR_STEPS_IMG])
+        for job in range(HEAD_JOBS // 2, HEAD_JOBS):
+            scalar_stats_img(job)
         next_chunk(0, 0)
 
         ALL_ROUNDS = STREAMS * ROUNDS
@@ -410,30 +432,30 @@ def tile_modalityadaptivemodule_pa_k_kernel(
             return HEAD_VECTOR + r * (VECTOR_JOBS[1] - HEAD_VECTOR) // STAT_ROUNDS
 
         def first_scalar(r):
-            return HEAD_JOBS + r * (SCALAR_JOBS - HEAD_JOBS) // STAT_ROUNDS
+            return HEAD_JOBS + r * (len(SCALAR_JOBS) - HEAD_JOBS) // STAT_ROUNDS
 
         img_steps = {
-            STAT_ROUNDS: (total_img, lambda: scalar_mean(1), lambda: mean_offset(1)),
-            STAT_ROUNDS + 1: (lambda: offset_excess(1), lambda: total_square(1), lambda: scalar_m2(1)),
-            STAT_ROUNDS + 2: (lambda: aggregate(1),),
-            STAT_ROUNDS + 3: (lambda: invert(1), lift_img),
+            STAT_ROUNDS: (None, None, mean_img, lambda: total_square(1)),
+            STAT_ROUNDS + 1: (None, lambda: mean_offset(1), lambda: offset_excess(1), lambda: scalar_m2(1)),
+            STAT_ROUNDS + 2: (lambda: aggregate(1), lambda: invert(1), lift_img),
         }
 
         def img_step(r, i):
             steps = img_steps.get(r, ())
-            if i < len(steps):
+            if i < len(steps) and steps[i]:
                 steps[i]()
 
         for r in range(ALL_ROUNDS + 5 + 1):
+            img_step(r, 0)
             if r < ALL_ROUNDS:
                 turn(r)
                 gain_shift(r)
             if 0 <= r - 2 < ALL_ROUNDS:
                 regroup(r - 2)
-            img_step(r, 0)
+            img_step(r, 1)
             if 0 <= r - 3 < ALL_ROUNDS:
                 quantise(r - 3)
-            img_step(r, 1)
+            img_step(r, 2)
             if (r + 1) % ROUNDS_PER_CHUNK == 0 and r + 1 < ALL_ROUNDS:
                 next_chunk(*divmod((r + 1) // ROUNDS_PER_CHUNK, CHUNKS))
             if r - 5 in (ROUNDS - 1, ALL_ROUNDS - 1):
@@ -451,4 +473,4 @@ def tile_modalityadaptivemodule_pa_k_kernel(
             if r == STAT_ROUNDS - 1:
                 load_scale_planes(1)
                 load_biases()
-            img_step(r, 2)
+            img_step(r, 3)

@@ -60,6 +60,7 @@ VECTOR_SLOTS = (PACK, PACK - 1)
 W_GROUPS = 4
 W_TILES = GROUPS // W_GROUPS
 W_BUFS = 4
+ALL_ROUNDS = STREAMS * ROUNDS
 ROUNDS_PER_W = W_GROUPS // ROUND_GROUPS
 
 FLOPS = 2 * 3 * STREAMS * ROWS * D * E
@@ -77,9 +78,9 @@ def tile_modalityadaptivemodule_pa_k_kernel(
 ):
     nc = tc.nc
     streams = (text, img)
-    words_of = ((Wq_words, Wkt_words, Wvt_words), (Wq_words, Wki_words, Wvi_words))
-    scales_of = ((Wq_scales, Wkt_scales, Wvt_scales), (Wq_scales, Wki_scales, Wvi_scales))
-    outs = (out_0, out_1, out_2)
+    words_of = ((Wkt_words, Wq_words, Wvt_words), (Wq_words, Wki_words, Wvi_words))
+    scales_of = ((Wkt_scales, Wq_scales, Wvt_scales), (Wq_scales, Wki_scales, Wvi_scales))
+    outs_of = ((out_1, out_0, out_2), (out_0, out_1, out_2))
 
     with ExitStack() as ctx:
         const = ctx.enter_context(tc.tile_pool(name="const", bufs=1))
@@ -134,12 +135,13 @@ def tile_modalityadaptivemodule_pa_k_kernel(
                         .bitcast(I32),
                     )
 
-        bias = const.tile([P, 5, E], BF16)
-        bias_slots = ((0, 1, 2), (0, 3, 4))
+        bias = const.tile([P, 5 * E], BF16)
+        pair_bias = (bias[:, 0 : 2 * E], bias[:, E : 3 * E])
+        v_bias = (bias[:, 3 * E : 4 * E], bias[:, 4 * E : 5 * E])
 
         def load_biases():
-            for slot, vector in enumerate((bq, bkt, bvt, bki, bvi)):
-                nc.sync.dma_start(out=bias[:, slot, :], in_=vector.partition_broadcast(P))
+            for slot, vector in enumerate((bkt, bq, bki, bvt, bvi)):
+                nc.sync.dma_start(out=bias[:, slot * E : (slot + 1) * E], in_=vector.partition_broadcast(P))
 
         gs_rows = const.tile([P, K_PASS], BF16)
         for v, vector in enumerate((ln_t_g, ln_t_b, ln_i_g, ln_i_b)):
@@ -151,7 +153,6 @@ def tile_modalityadaptivemodule_pa_k_kernel(
         make_identity(nc, identity[:])
         identity_bf = const.tile([P, P], BF16)
         nc.gpsimd.tensor_copy(out=identity_bf[:], in_=identity[:])
-        nc.gpsimd.memset(w_planes[1][:].rearrange("p g n -> p (g n)").bitcast(I32), 0)
 
         for c in range(CHUNKS):
             load_x(0, c, pieces=4 if c == 0 else 2)
@@ -163,6 +164,7 @@ def tile_modalityadaptivemodule_pa_k_kernel(
 
         gs_sorted = const.tile([P, PACK, P], F32)
         nc.gpsimd.tensor_copy(out=gs_sorted[:], in_=gs_rows[:].rearrange("q (p t) -> q t p", t=PACK))
+        nc.gpsimd.memset(w_planes[1][:].rearrange("p g n -> p (g n)").bitcast(I32), 0)
         gs_cols = const.tile([P, PACK, P], F32)
 
         tuples = [const.tile([P, TILES, TUPLES[s] + 1, 3], F32, name="tuples%d" % s) for s in range(STREAMS)]
@@ -318,37 +320,39 @@ def tile_modalityadaptivemodule_pa_k_kernel(
             planes = work.tile([P, PACK, ROUND_GROUPS * ROWS], BF16, bufs=3)
             for gl in range(ROUND_GROUPS):
                 g = i * ROUND_GROUPS + gl
-                for half in range(PACK // 2):
-                    for u in range(2):
-                        t = 2 * half + u
-                        nc.scalar.activation(
-                            out=planes[:, t, gl * ROWS : (gl + 1) * ROWS],
-                            in_=banks[(r, gl, half)][:, u, :],
-                            func=ACT.Identity,
-                            scale=gs_cols[:, t, 2 * s * GROUPS + g : 2 * s * GROUPS + g + 1],
-                            bias=gs_cols[:, t, (2 * s + 1) * GROUPS + g : (2 * s + 1) * GROUPS + g + 1],
-                        )
+                for t in range(PACK):
+                    nc.scalar.activation(
+                        out=planes[:, t, gl * ROWS : (gl + 1) * ROWS],
+                        in_=banks[(r, gl, t // 2)][:, t % 2, :],
+                        func=ACT.Identity,
+                        scale=gs_cols[:, t, 2 * s * GROUPS + g : 2 * s * GROUPS + g + 1],
+                        bias=gs_cols[:, t, (2 * s + 1) * GROUPS + g : (2 * s + 1) * GROUPS + g + 1],
+                    )
             planes_of[r] = planes
 
-        def regroup(r):
-            grouped = work.tile([P, ROUND_GROUPS * ROWS, PACK], BF16, align_bytes=64)
+        def regroup(r, first=0, last=ROUND_GROUPS):
+            if r not in grouped_of:
+                grouped = work.tile([P, ROUND_GROUPS * ROWS, PACK], BF16, align_bytes=64)
+                grouped_of[r] = grouped
+            cols = slice(first * ROWS, last * ROWS)
             nc.vector.tensor_copy(
-                out=grouped[:].rearrange("p (c i) t -> p c t i", i=4),
-                in_=planes_of[r][:].rearrange("p t (c i) -> p c t i", i=4),
+                out=grouped_of[r][:, cols, :].rearrange("p (c i) t -> p c t i", i=4),
+                in_=planes_of[r][:, :, cols].rearrange("p t (c i) -> p c t i", i=4),
             )
-            grouped_of[r] = grouped
 
-        def quantise(r):
-            codes = mx_pool.tile([P, ROUND_GROUPS * ROWS], U32, align_bytes=64)
-            code_scales = mx_pool.tile([P, ROUND_GROUPS * ROWS], U8, align_bytes=64)
+        def quantise(r, first=0, last=ROUND_GROUPS):
+            if r not in codes_of:
+                codes = mx_pool.tile([P, ROUND_GROUPS * ROWS], U32, align_bytes=64)
+                code_scales = mx_pool.tile([P, ROUND_GROUPS * ROWS], U8, align_bytes=64)
+                codes_of[r] = (codes, code_scales)
+            cols = slice(first * ROWS, last * ROWS)
             nc.vector.quantize_mx(
-                out=codes[:].bitcast(FP8X4),
-                scales=code_scales[:],
-                in_=grouped_of[r][:].rearrange("p c t -> p (c t)"),
+                out=codes_of[r][0][:, cols].bitcast(FP8X4),
+                scales=codes_of[r][1][:, cols],
+                in_=grouped_of[r][:, cols, :].rearrange("p c t -> p (c t)"),
             )
-            codes_of[r] = (codes, code_scales)
 
-        def multiply(r):
+        def multiply(r, gls=range(ROUND_GROUPS)):
             s, i = divmod(r, ROUNDS)
             if i == 0:
                 for j in range(TILES):
@@ -356,7 +360,7 @@ def tile_modalityadaptivemodule_pa_k_kernel(
                     acc_v = acc_psum.tile([P, E], F32, name="acc_v%d" % j)
                     acc_of[(s, j)] = (acc_qk, acc_v)
             codes, code_scales = codes_of[r]
-            for gl in range(ROUND_GROUPS):
+            for gl in gls:
                 g = i * ROUND_GROUPS + gl
                 w_tile = w_tiles[(s, g // W_GROUPS)]
                 for j in range(TILES):
@@ -376,31 +380,29 @@ def tile_modalityadaptivemodule_pa_k_kernel(
             result = work.tile([P, TILES, 3 * E], F32)
             for j in range(TILES):
                 acc_qk, acc_v = acc_of[(s, j)]
-                products = (acc_qk[:, 0:E], acc_qk[:, E : 2 * E], acc_v[:])
-                for i, product in enumerate(products):
-                    nc.vector.tensor_tensor(
-                        out=result[:, j, i * E : (i + 1) * E], in0=product,
-                        in1=bias[:, bias_slots[s][i], :], op=ALU.add,
-                    )
-            for i, out in enumerate(outs):
-                nc.sync.dma_start(
+                nc.vector.tensor_tensor(out=result[:, j, 0 : 2 * E], in0=acc_qk[:], in1=pair_bias[s], op=ALU.add)
+                nc.vector.tensor_tensor(out=result[:, j, 2 * E :], in0=acc_v[:], in1=v_bias[s], op=ALU.add)
+            for i, out in enumerate(outs_of[s]):
+                queue = nc.scalar if s == 1 and i == 1 else nc.sync
+                queue.dma_start(
                     out=out[TILES * s : TILES * (s + 1)].rearrange("b r n -> r b n"),
                     in_=result[:, :, i * E : (i + 1) * E],
                 )
 
-        gs_bank = turn_psum.tile([P, PACK, P], F32, tag="bank")
-        for t in range(PACK):
-            nc.tensor.transpose(gs_bank[:, t, :], gs_sorted[:, t, :], identity[:])
         UNIT_JOBS = TILES * UNIT_BLOCKS
         open_sums(0)
         for step in range(STEPS):
             for job in range(step * UNIT_JOBS, (step + 1) * UNIT_JOBS):
                 vector_stats(0, job)
-            if step == 1:
-                nc.vector.tensor_copy(out=gs_cols[:], in_=gs_bank[:])
             for j in range(TILES):
                 square(0, step, j)
                 add_up_on_tensor(0, step, j, STEPS)
+            if step == STEPS - 3:
+                gs_bank = turn_psum.tile([P, PACK, P], F32, tag="bank")
+                for t in range(PACK):
+                    nc.tensor.transpose(gs_bank[:, t, :], gs_sorted[:, t, :], identity[:])
+            if step == STEPS - 2:
+                nc.vector.tensor_copy(out=gs_cols[:], in_=gs_bank[:])
         add_up_bank(0, tuples[0][:, :, TUPLES[0], 1:2])
         open_sums(1)
         for step in range(TENSOR_STEPS_IMG):
@@ -425,7 +427,6 @@ def tile_modalityadaptivemodule_pa_k_kernel(
             scalar_stats_img(job)
         next_chunk(0, 0)
 
-        ALL_ROUNDS = STREAMS * ROUNDS
         STAT_ROUNDS = 12
 
         def first_vector(r):
@@ -445,22 +446,21 @@ def tile_modalityadaptivemodule_pa_k_kernel(
             if i < len(steps) and steps[i]:
                 steps[i]()
 
-        for r in range(ALL_ROUNDS + 5 + 1):
+        for r in range(ALL_ROUNDS):
             img_step(r, 0)
-            if r < ALL_ROUNDS:
-                turn(r)
-                gain_shift(r)
-            if 0 <= r - 2 < ALL_ROUNDS:
+            turn(r)
+            gain_shift(r)
+            if r >= 2:
                 regroup(r - 2)
             img_step(r, 1)
-            if 0 <= r - 3 < ALL_ROUNDS:
+            if r >= 3:
                 quantise(r - 3)
             img_step(r, 2)
             if (r + 1) % ROUNDS_PER_CHUNK == 0 and r + 1 < ALL_ROUNDS:
                 next_chunk(*divmod((r + 1) // ROUNDS_PER_CHUNK, CHUNKS))
-            if r - 5 in (ROUNDS - 1, ALL_ROUNDS - 1):
-                finish((r - 5) // ROUNDS)
-            if 0 <= r - 4 < ALL_ROUNDS:
+            if r - 5 == ROUNDS - 1:
+                finish(0)
+            if r >= 4:
                 multiply(r - 4)
                 h = (r - 4) // ROUNDS_PER_W + W_BUFS
                 if (r - 4) % ROUNDS_PER_W == ROUNDS_PER_W - 1 and h < STREAMS * W_TILES:
@@ -474,3 +474,18 @@ def tile_modalityadaptivemodule_pa_k_kernel(
                 load_scale_planes(1)
                 load_biases()
             img_step(r, 3)
+
+        last = ALL_ROUNDS - 1
+        multiply(last - 3)
+        regroup(last - 1)
+        quantise(last - 2)
+        multiply(last - 2)
+        regroup(last, 0, 1)
+        quantise(last - 1)
+        multiply(last - 1)
+        regroup(last, 1, 2)
+        quantise(last, 0, 1)
+        multiply(last, [0])
+        quantise(last, 1, 2)
+        multiply(last, [1])
+        finish(1)

@@ -48,8 +48,8 @@ SCALAR_JOBS = [
     for square in ((True,) if step < TENSOR_STEPS_IMG else (False, True))
     for j in range(TILES)
 ]
-HEAD_JOBS = 4
-HEAD_VECTOR = 4
+HEAD_JOBS = 2
+HEAD_VECTOR = 2
 
 ROUND_GROUPS = 2
 ROUND_COLS = ROUND_GROUPS * K_PASS
@@ -155,7 +155,7 @@ def tile_modalityadaptivemodule_pa_k_kernel(
         nc.gpsimd.tensor_copy(out=identity_bf[:], in_=identity[:])
 
         for c in range(CHUNKS):
-            load_x(0, c, pieces=4 if c == 0 else 2)
+            load_x(0, c, pieces=2 if c in (0, CHUNKS - 1) else 1)
         for c in range(X_BUFS - CHUNKS):
             load_x(1, c)
         load_scale_planes(0)
@@ -208,18 +208,18 @@ def tile_modalityadaptivemodule_pa_k_kernel(
             )
 
         def add_up_on_tensor(s, step, j, steps):
-            for b in range(UNIT // P):
+            for b in range(UNIT_BLOCKS):
                 nc.tensor.matmul(
                     sum_banks[(s, j)][:], lhsT=identity_bf[:],
-                    rhs=unit_rows(s, UNITS_OF[s][1][step], j)[:, b * P : (b + 1) * P],
-                    start=(step == 0 and b == 0), stop=(step == steps - 1 and b == UNIT // P - 1),
+                    rhs=unit_rows(s, UNITS_OF[s][1][step], j)[:, b * STAT_BLOCK : (b + 1) * STAT_BLOCK],
+                    start=(step == 0 and b == 0), stop=(step == steps - 1 and b == UNIT_BLOCKS - 1),
                 )
 
         def add_up_bank(s, out):
             for j in range(TILES):
                 unread = work.tile([P, UNIT], BF16)
                 nc.scalar.activation(
-                    out=unread[:, 0:P], in_=sum_banks[(s, j)][:], func=ACT.Identity, scale=1.0 / SCALAR_COLS[s],
+                    out=unread[:, 0:STAT_BLOCK], in_=sum_banks[(s, j)][:], func=ACT.Identity, scale=1.0 / SCALAR_COLS[s],
                     accum_out=out[:, j, :],
                 )
 
@@ -227,7 +227,7 @@ def tile_modalityadaptivemodule_pa_k_kernel(
 
         def open_sums(s):
             for j in range(TILES):
-                sum_bank = turn_psum.tile([P, P], F32, tag="bank")
+                sum_bank = turn_psum.tile([P, STAT_BLOCK], F32, tag="bank")
                 sum_banks[(s, j)] = sum_bank
 
         def scalar_stats_img(job):
@@ -411,19 +411,14 @@ def tile_modalityadaptivemodule_pa_k_kernel(
         text_steps = [total_square, mean_offset, offset_excess, scalar_m2]
         for job in range(STEPS * UNIT_JOBS, VECTOR_JOBS[0]):
             vector_stats(0, job)
-            if job == VECTOR_JOBS[0] - 2 - len(text_steps):
-                for img_job in range(HEAD_VECTOR // 2):
-                    vector_stats(1, img_job)
             if job > VECTOR_JOBS[0] - 2 - len(text_steps) and text_steps:
                 text_steps.pop(0)(0)
-        for job in range(HEAD_JOBS // 2):
-            scalar_stats_img(job)
         aggregate(0)
-        for job in range(HEAD_VECTOR // 2, HEAD_VECTOR):
+        for job in range(HEAD_VECTOR):
             vector_stats(1, job)
         invert(0)
         add_up_bank(1, sums[:, :, TENSOR_STEPS_IMG - 1 : TENSOR_STEPS_IMG])
-        for job in range(HEAD_JOBS // 2, HEAD_JOBS):
+        for job in range(HEAD_JOBS):
             scalar_stats_img(job)
         next_chunk(0, 0)
 

@@ -145,7 +145,7 @@ def tile_modalityadaptivemodule_pa_k_kernel(
 
         gs_rows = const.tile([P, K_PASS], BF16)
         for v, vector in enumerate((ln_t_g, ln_t_b, ln_i_g, ln_i_b)):
-            nc.gpsimd.dma_start(
+            nc.sync.dma_start(
                 out=gs_rows[v * GROUPS : (v + 1) * GROUPS, :],
                 in_=vector.rearrange("(g c) -> g c", c=K_PASS),
             )

@@ -35,7 +35,7 @@ SCALAR_UNITS = [u for u in range(UNITS - 2) if u % 2 == 1]
 VECTOR_UNITS = [u for u in range(UNITS) if u not in SCALAR_UNITS]
 UNIT_BLOCKS = UNIT // STAT_BLOCK
 STEPS = len(SCALAR_UNITS)
-SCALAR_UNITS_IMG = [1, 3, 5, 7, 9, 11]
+SCALAR_UNITS_IMG = [1, 3, 5, 7, 9, 11, 13]
 TENSOR_STEPS_IMG = 2
 VECTOR_UNITS_IMG = [u for u in range(UNITS) if u not in SCALAR_UNITS_IMG]
 UNITS_OF = ((VECTOR_UNITS, SCALAR_UNITS), (VECTOR_UNITS_IMG, SCALAR_UNITS_IMG))
@@ -123,7 +123,6 @@ def tile_modalityadaptivemodule_pa_k_kernel(
             w_tiles[(s, h)] = w_tile
 
         w_planes = [const.tile([P, GROUPS, 3 * E], U8, align_bytes=64, name="w_plane%d" % s) for s in range(STREAMS)]
-        nc.vector.memset(w_planes[0][:].rearrange("p g n -> p (g n)").bitcast(I32), 0)
 
         def load_scale_planes(s):
             for i, scales in enumerate(scales_of[s]):
@@ -153,6 +152,7 @@ def tile_modalityadaptivemodule_pa_k_kernel(
         make_identity(nc, identity[:])
         identity_bf = const.tile([P, P], BF16)
         nc.gpsimd.tensor_copy(out=identity_bf[:], in_=identity[:])
+        nc.gpsimd.memset(w_planes[0][:].rearrange("p g n -> p (g n)").bitcast(I32), 0)
 
         for c in range(CHUNKS):
             load_x(0, c, pieces=2 if c in (0, CHUNKS - 1) else 1)
@@ -277,7 +277,7 @@ def tile_modalityadaptivemodule_pa_k_kernel(
             xs = work.tile([P, TILES, CHUNK_GROUPS, PACK, P], F32)
             sorted_x[(s, c)] = xs
             for part, j in [(part, j) for part in range(parts) for j in range(TILES)]:
-                cut = VECTOR_SLOTS[s] if j == TILES - 1 else PACK
+                cut = VECTOR_SLOTS[s]
                 gs = slice(part * CHUNK_GROUPS // parts, (part + 1) * CHUNK_GROUPS // parts)
                 x_sorted = x_chunks[(s, c)][:, j, :].rearrange("r (g p t) -> r g t p", p=P, t=PACK)
                 nc.vector.tensor_scalar(

@@ -31,12 +31,15 @@ STAT_BLOCK = 512
 
 UNIT = CHUNK // 2
 UNITS = D // UNIT
-SCALAR_UNITS = [u for u in range(UNITS - 2) if u % 2 == 1]
+SCALAR_UNITS = [u for u in range(UNITS - 2) if u % 2 == 1] + [UNITS - 2]
 VECTOR_UNITS = [u for u in range(UNITS) if u not in SCALAR_UNITS]
 UNIT_BLOCKS = UNIT // STAT_BLOCK
 STEPS = len(SCALAR_UNITS)
+GPSIMD_STEPS = (1, 3, 5)
 SCALAR_UNITS_IMG = [1, 3, 5, 7, 9, 11, 13]
-TENSOR_STEPS_IMG = 2
+TENSOR_BATCHES = ((0, (1, 2)), (7, (3, 4)))
+TENSOR_STEPS = [step for r, steps in TENSOR_BATCHES for step in steps]
+SUM_STEPS = [step for step in range(len(SCALAR_UNITS_IMG)) if step not in TENSOR_STEPS]
 VECTOR_UNITS_IMG = [u for u in range(UNITS) if u not in SCALAR_UNITS_IMG]
 UNITS_OF = ((VECTOR_UNITS, SCALAR_UNITS), (VECTOR_UNITS_IMG, SCALAR_UNITS_IMG))
 SCALAR_COLS = [UNIT * len(scalar_units) for vector_units, scalar_units in UNITS_OF]
@@ -45,11 +48,11 @@ VECTOR_JOBS = [TILES * UNIT_BLOCKS * len(vector_units) for vector_units, scalar_
 SCALAR_JOBS = [
     (square, step, j)
     for step in range(len(SCALAR_UNITS_IMG))
-    for square in ((True,) if step < TENSOR_STEPS_IMG else (False, True))
+    for square in ((False, True) if step in SUM_STEPS else (True,))
     for j in range(TILES)
 ]
-HEAD_JOBS = 2
-HEAD_VECTOR = 2
+HEAD_JOBS = 4
+HEAD_VECTOR = 4
 
 ROUND_GROUPS = 2
 ROUND_COLS = ROUND_GROUPS * K_PASS
@@ -152,24 +155,20 @@ def tile_modalityadaptivemodule_pa_k_kernel(
         make_identity(nc, identity[:])
         identity_bf = const.tile([P, P], BF16)
         nc.gpsimd.tensor_copy(out=identity_bf[:], in_=identity[:])
-        nc.gpsimd.memset(w_planes[0][:].rearrange("p g n -> p (g n)").bitcast(I32), 0)
 
         for c in range(CHUNKS):
             load_x(0, c, pieces=2 if c in (0, CHUNKS - 1) else 1)
         for c in range(X_BUFS - CHUNKS):
             load_x(1, c)
-        load_scale_planes(0)
-        for h in range(W_BUFS):
-            load_weights(0, h)
 
         gs_sorted = const.tile([P, PACK, P], F32)
         nc.gpsimd.tensor_copy(out=gs_sorted[:], in_=gs_rows[:].rearrange("q (p t) -> q t p", t=PACK))
-        nc.gpsimd.memset(w_planes[1][:].rearrange("p g n -> p (g n)").bitcast(I32), 0)
         gs_cols = const.tile([P, PACK, P], F32)
 
         tuples = [const.tile([P, TILES, TUPLES[s] + 1, 3], F32, name="tuples%d" % s) for s in range(STREAMS)]
         squares = [const.tile([P, TILES, len(UNITS_OF[s][1])], F32, name="squares%d" % s) for s in range(STREAMS)]
-        sums = const.tile([P, TILES, len(SCALAR_UNITS_IMG)], F32)
+        sums = const.tile([P, TILES, len(SUM_STEPS) + len(TENSOR_BATCHES)], F32)
+        gpsimd_sums = [const.tile([P, STAT_BLOCK], F32, name="gpsimd_sum%d" % j) for j in range(TILES)]
         offset = [const.tile([P, TILES], F32, name="offset%d" % s) for s in range(STREAMS)]
         excess = [const.tile([P, TILES], F32, name="excess%d" % s) for s in range(STREAMS)]
         square_sum = [const.tile([P, TILES], F32, name="square_sum%d" % s) for s in range(STREAMS)]
@@ -204,31 +203,56 @@ def tile_modalityadaptivemodule_pa_k_kernel(
             unread = work.tile([P, UNIT], BF16)
             nc.scalar.activation(
                 out=unread[:], in_=unit_rows(s, UNITS_OF[s][1][step], j), func=ACT.Identity,
-                scale=1.0 / SCALAR_COLS[s], accum_out=sums[:, j, step : step + 1],
+                scale=1.0 / SCALAR_COLS[s], accum_out=sums[:, j, SUM_STEPS.index(step) : SUM_STEPS.index(step) + 1],
             )
 
-        def add_up_on_tensor(s, step, j, steps):
+        def add_up_text(step, j):
             for b in range(UNIT_BLOCKS):
-                nc.tensor.matmul(
-                    sum_banks[(s, j)][:], lhsT=identity_bf[:],
-                    rhs=unit_rows(s, UNITS_OF[s][1][step], j)[:, b * STAT_BLOCK : (b + 1) * STAT_BLOCK],
-                    start=(step == 0 and b == 0), stop=(step == steps - 1 and b == UNIT_BLOCKS - 1),
-                )
+                block = unit_rows(0, SCALAR_UNITS[step], j)[:, b * STAT_BLOCK : (b + 1) * STAT_BLOCK]
+                if step not in GPSIMD_STEPS:
+                    nc.tensor.matmul(
+                        sum_banks[j][:], lhsT=identity_bf[:], rhs=block, start=(step == 0 and b == 0), stop=False
+                    )
+                elif step > GPSIMD_STEPS[0]:
+                    nc.gpsimd.tensor_tensor(out=gpsimd_sums[j][:], in0=gpsimd_sums[j][:], in1=block, op=ALU.add)
+                elif b == 0:
+                    first_block = block
+                else:
+                    nc.gpsimd.tensor_tensor(out=gpsimd_sums[j][:], in0=first_block, in1=block, op=ALU.add)
+            if step == STEPS - 1:
+                nc.tensor.matmul(sum_banks[j][:], lhsT=identity[:], rhs=gpsimd_sums[j][:], start=False, stop=True)
 
-        def add_up_bank(s, out):
+        def mean_text():
             for j in range(TILES):
                 unread = work.tile([P, UNIT], BF16)
                 nc.scalar.activation(
-                    out=unread[:, 0:STAT_BLOCK], in_=sum_banks[(s, j)][:], func=ACT.Identity, scale=1.0 / SCALAR_COLS[s],
-                    accum_out=out[:, j, :],
+                    out=unread[:, 0:STAT_BLOCK], in_=sum_banks[j][:], func=ACT.Identity, scale=1.0 / SCALAR_COLS[0],
+                    accum_out=tuples[0][:, j, TUPLES[0], 1:2],
                 )
 
-        sum_banks = {}
+        HALF = STAT_BLOCK // 2
+        batch_banks = {}
 
-        def open_sums(s):
+        def add_up_batch(batch):
+            steps = TENSOR_BATCHES[batch][1]
+            batch_bank = turn_psum.tile([P, TILES, HALF], F32, tag="bank")
+            batch_banks[batch] = batch_bank
             for j in range(TILES):
-                sum_bank = turn_psum.tile([P, STAT_BLOCK], F32, tag="bank")
-                sum_banks[(s, j)] = sum_bank
+                for step in steps:
+                    rows = unit_rows(1, SCALAR_UNITS_IMG[step], j)
+                    for b in range(UNIT // HALF):
+                        nc.tensor.matmul(
+                            batch_bank[:, j, :], lhsT=identity_bf[:], rhs=rows[:, b * HALF : (b + 1) * HALF],
+                            start=(step == steps[0] and b == 0), stop=(step == steps[-1] and b == UNIT // HALF - 1),
+                        )
+
+        def mean_batch(batch):
+            for j in range(TILES):
+                unread = work.tile([P, UNIT], BF16)
+                nc.scalar.activation(
+                    out=unread[:, 0:HALF], in_=batch_banks[batch][:, j, :], func=ACT.Identity, scale=1.0 / SCALAR_COLS[1],
+                    accum_out=sums[:, j, len(SUM_STEPS) + batch : len(SUM_STEPS) + batch + 1],
+                )
 
         def scalar_stats_img(job):
             squared, step, j = SCALAR_JOBS[job]
@@ -236,7 +260,7 @@ def tile_modalityadaptivemodule_pa_k_kernel(
 
         def mean_img():
             nc.vector.tensor_reduce(
-                out=tuples[1][:, :, TUPLES[1], 1], in_=sums[:, :, TENSOR_STEPS_IMG - 1 :], axis=AXIS.X, op=ALU.add
+                out=tuples[1][:, :, TUPLES[1], 1], in_=sums[:], axis=AXIS.X, op=ALU.add
             )
 
         def mean_offset(s):
@@ -277,7 +301,7 @@ def tile_modalityadaptivemodule_pa_k_kernel(
             xs = work.tile([P, TILES, CHUNK_GROUPS, PACK, P], F32)
             sorted_x[(s, c)] = xs
             for part, j in [(part, j) for part in range(parts) for j in range(TILES)]:
-                cut = VECTOR_SLOTS[s]
+                cut = VECTOR_SLOTS[s] if j == TILES - 1 else PACK
                 gs = slice(part * CHUNK_GROUPS // parts, (part + 1) * CHUNK_GROUPS // parts)
                 x_sorted = x_chunks[(s, c)][:, j, :].rearrange("r (g p t) -> r g t p", p=P, t=PACK)
                 nc.vector.tensor_scalar(
@@ -390,39 +414,38 @@ def tile_modalityadaptivemodule_pa_k_kernel(
                 )
 
         UNIT_JOBS = TILES * UNIT_BLOCKS
-        open_sums(0)
+        sum_banks = [turn_psum.tile([P, STAT_BLOCK], F32, tag="bank", name="sum_bank%d" % j) for j in range(TILES)]
         for step in range(STEPS):
             for job in range(step * UNIT_JOBS, (step + 1) * UNIT_JOBS):
                 vector_stats(0, job)
             for j in range(TILES):
                 square(0, step, j)
-                add_up_on_tensor(0, step, j, STEPS)
+                add_up_text(step, j)
             if step == STEPS - 3:
                 gs_bank = turn_psum.tile([P, PACK, P], F32, tag="bank")
                 for t in range(PACK):
                     nc.tensor.transpose(gs_bank[:, t, :], gs_sorted[:, t, :], identity[:])
             if step == STEPS - 2:
                 nc.vector.tensor_copy(out=gs_cols[:], in_=gs_bank[:])
-        add_up_bank(0, tuples[0][:, :, TUPLES[0], 1:2])
-        open_sums(1)
-        for step in range(TENSOR_STEPS_IMG):
-            for j in range(TILES):
-                add_up_on_tensor(1, step, j, TENSOR_STEPS_IMG)
+        for s in range(STREAMS):
+            nc.gpsimd.memset(w_planes[s][:].rearrange("p g n -> p (g n)").bitcast(I32), 0)
+        load_scale_planes(0)
+        for h in range(W_BUFS):
+            load_weights(0, h)
+        mean_text()
         text_steps = [total_square, mean_offset, offset_excess, scalar_m2]
-        for job in range(STEPS * UNIT_JOBS, VECTOR_JOBS[0]):
-            vector_stats(0, job)
-            if job > VECTOR_JOBS[0] - 2 - len(text_steps) and text_steps:
-                text_steps.pop(0)(0)
-        aggregate(0)
         for job in range(HEAD_VECTOR):
+            text_steps[job](0)
             vector_stats(1, job)
+        for job in range(HEAD_JOBS // 2):
+            scalar_stats_img(job)
+        aggregate(0)
         invert(0)
-        add_up_bank(1, sums[:, :, TENSOR_STEPS_IMG - 1 : TENSOR_STEPS_IMG])
-        for job in range(HEAD_JOBS):
+        for job in range(HEAD_JOBS // 2, HEAD_JOBS):
             scalar_stats_img(job)
         next_chunk(0, 0)
 
-        STAT_ROUNDS = 12
+        STAT_ROUNDS = 13
 
         def first_vector(r):
             return HEAD_VECTOR + r * (VECTOR_JOBS[1] - HEAD_VECTOR) // STAT_ROUNDS
@@ -445,6 +468,11 @@ def tile_modalityadaptivemodule_pa_k_kernel(
             img_step(r, 0)
             turn(r)
             gain_shift(r)
+            for batch in range(len(TENSOR_BATCHES)):
+                if r == TENSOR_BATCHES[batch][0]:
+                    add_up_batch(batch)
+                if r == TENSOR_BATCHES[batch][0] + 1:
+                    mean_batch(batch)
             if r >= 2:
                 regroup(r - 2)
             img_step(r, 1)

@@ -35,9 +35,11 @@ SCALAR_UNITS = [u for u in range(UNITS - 2) if u % 2 == 1] + [UNITS - 2]
 VECTOR_UNITS = [u for u in range(UNITS) if u not in SCALAR_UNITS]
 UNIT_BLOCKS = UNIT // STAT_BLOCK
 STEPS = len(SCALAR_UNITS)
-GPSIMD_STEPS = (1, 3, 5)
+GPSIMD_STEPS = (0, 1, 3)
+GPSIMD_TAKEN = 5
+TENSOR_TEXT_STEPS = [step for step in range(STEPS) if step not in GPSIMD_STEPS]
 SCALAR_UNITS_IMG = [1, 3, 5, 7, 9, 11, 13]
-TENSOR_BATCHES = ((0, (1, 2)), (7, (3, 4)))
+TENSOR_BATCHES = ((0, (1, 2)), (6, (3, 4)))
 TENSOR_STEPS = [step for r, steps in TENSOR_BATCHES for step in steps]
 SUM_STEPS = [step for step in range(len(SCALAR_UNITS_IMG)) if step not in TENSOR_STEPS]
 VECTOR_UNITS_IMG = [u for u in range(UNITS) if u not in SCALAR_UNITS_IMG]
@@ -59,7 +61,7 @@ ROUND_COLS = ROUND_GROUPS * K_PASS
 ROUNDS = GROUPS // ROUND_GROUPS
 ROUNDS_PER_CHUNK = CHUNK // ROUND_COLS
 CHUNK_GROUPS = CHUNK // K_PASS
-VECTOR_SLOTS = (PACK, PACK - 1)
+SCALAR_CHUNKS = (range(6, CHUNKS), range(CHUNKS))
 W_GROUPS = 4
 W_TILES = GROUPS // W_GROUPS
 W_BUFS = 4
@@ -90,7 +92,7 @@ def tile_modalityadaptivemodule_pa_k_kernel(
         x_pool = ctx.enter_context(tc.tile_pool(name="x", bufs=X_BUFS))
         w_pool = ctx.enter_context(tc.tile_pool(name="w", bufs=W_BUFS))
         work = ctx.enter_context(tc.tile_pool(name="work", bufs=2))
-        mx_pool = ctx.enter_context(tc.tile_pool(name="mx", bufs=3))
+        mx_pool = ctx.enter_context(tc.tile_pool(name="mx", bufs=2))
         turn_psum = ctx.enter_context(tc.psum_pool(name="turn", bufs=4))
         acc_psum = ctx.enter_context(tc.psum_pool(name="acc", bufs=1))
         ctx.enter_context(tc.manual_schedule())
@@ -106,6 +108,8 @@ def tile_modalityadaptivemodule_pa_k_kernel(
             x_chunk = x_pool.tile([P, TILES, CHUNK], BF16)
             width = CHUNK // pieces
             for i in range(pieces):
+                if (s, c, i) == (0, 0, 1):
+                    load_gains()
                 nc.sync.dma_start(
                     out=x_chunk[:, :, i * width : (i + 1) * width],
                     in_=streams[s].rearrange("b r d -> r b d")[:, :, c * CHUNK + i * width : c * CHUNK + (i + 1) * width],
@@ -146,11 +150,14 @@ def tile_modalityadaptivemodule_pa_k_kernel(
                 nc.sync.dma_start(out=bias[:, slot * E : (slot + 1) * E], in_=vector.partition_broadcast(P))
 
         gs_rows = const.tile([P, K_PASS], BF16)
-        for v, vector in enumerate((ln_t_g, ln_t_b, ln_i_g, ln_i_b)):
-            nc.sync.dma_start(
-                out=gs_rows[v * GROUPS : (v + 1) * GROUPS, :],
-                in_=vector.rearrange("(g c) -> g c", c=K_PASS),
-            )
+
+        def load_gains():
+            for v, vector in enumerate((ln_t_g, ln_t_b, ln_i_g, ln_i_b)):
+                nc.sync.dma_start(
+                    out=gs_rows[v * GROUPS : (v + 1) * GROUPS, :],
+                    in_=vector.rearrange("(g c) -> g c", c=K_PASS),
+                )
+
         identity = const.tile([P, P], F32)
         make_identity(nc, identity[:])
         identity_bf = const.tile([P, P], BF16)
@@ -162,7 +169,7 @@ def tile_modalityadaptivemodule_pa_k_kernel(
             load_x(1, c)
 
         gs_sorted = const.tile([P, PACK, P], F32)
-        nc.gpsimd.tensor_copy(out=gs_sorted[:], in_=gs_rows[:].rearrange("q (p t) -> q t p", t=PACK))
+        nc.scalar.copy(out=gs_sorted[:], in_=gs_rows[:].rearrange("q (p t) -> q t p", t=PACK))
         gs_cols = const.tile([P, PACK, P], F32)
 
         tuples = [const.tile([P, TILES, TUPLES[s] + 1, 3], F32, name="tuples%d" % s) for s in range(STREAMS)]
@@ -175,7 +182,7 @@ def tile_modalityadaptivemodule_pa_k_kernel(
         mean_var = [const.tile([P, TILES, 2], F32, name="mean_var%d" % s) for s in range(STREAMS)]
         std = [const.tile([P, TILES], F32, name="std%d" % s) for s in range(STREAMS)]
         rstd = [const.tile([P, TILES], F32, name="rstd%d" % s) for s in range(STREAMS)]
-        lift = const.tile([P, TILES], F32)
+        lift = [const.tile([P, TILES], F32, name="lift%d" % s) for s in range(STREAMS)]
 
         for s in range(STREAMS):
             nc.vector.memset(tuples[s][:, :, TUPLES[s], 0], float(SCALAR_COLS[s]))
@@ -206,21 +213,22 @@ def tile_modalityadaptivemodule_pa_k_kernel(
                 scale=1.0 / SCALAR_COLS[s], accum_out=sums[:, j, SUM_STEPS.index(step) : SUM_STEPS.index(step) + 1],
             )
 
-        def add_up_text(step, j):
+        def add_up_text(step):
             for b in range(UNIT_BLOCKS):
-                block = unit_rows(0, SCALAR_UNITS[step], j)[:, b * STAT_BLOCK : (b + 1) * STAT_BLOCK]
-                if step not in GPSIMD_STEPS:
-                    nc.tensor.matmul(
-                        sum_banks[j][:], lhsT=identity_bf[:], rhs=block, start=(step == 0 and b == 0), stop=False
-                    )
-                elif step > GPSIMD_STEPS[0]:
-                    nc.gpsimd.tensor_tensor(out=gpsimd_sums[j][:], in0=gpsimd_sums[j][:], in1=block, op=ALU.add)
-                elif b == 0:
-                    first_block = block
-                else:
-                    nc.gpsimd.tensor_tensor(out=gpsimd_sums[j][:], in0=first_block, in1=block, op=ALU.add)
-            if step == STEPS - 1:
-                nc.tensor.matmul(sum_banks[j][:], lhsT=identity[:], rhs=gpsimd_sums[j][:], start=False, stop=True)
+                for j in range(TILES):
+                    rows = unit_rows(0, SCALAR_UNITS[step], j)
+                    block = rows[:, b * STAT_BLOCK : (b + 1) * STAT_BLOCK]
+                    if step not in GPSIMD_STEPS:
+                        first = step == TENSOR_TEXT_STEPS[0] and b == 0
+                        last = step == STEPS - 1 and b == UNIT_BLOCKS - 1
+                        nc.tensor.matmul(sum_banks[j][:], lhsT=identity_bf[:], rhs=block, start=first, stop=last)
+                    elif step > GPSIMD_STEPS[0]:
+                        nc.gpsimd.tensor_tensor(out=gpsimd_sums[j][:], in0=gpsimd_sums[j][:], in1=block, op=ALU.add)
+                    elif b == 1:
+                        nc.gpsimd.tensor_tensor(out=gpsimd_sums[j][:], in0=rows[:, :STAT_BLOCK], in1=block, op=ALU.add)
+            if step == GPSIMD_TAKEN:
+                for j in range(TILES):
+                    nc.tensor.matmul(sum_banks[j][:], lhsT=identity[:], rhs=gpsimd_sums[j][:], start=False, stop=False)
 
         def mean_text():
             for j in range(TILES):
@@ -285,9 +293,9 @@ def tile_modalityadaptivemodule_pa_k_kernel(
         def invert(s):
             nc.vector.reciprocal(out=rstd[s][:], in_=std[s][:])
 
-        def lift_img():
+        def lift_rows(s):
             nc.vector.scalar_tensor_tensor(
-                out=lift[:], in0=mean_var[1][:, :, 0], scalar=-1.0, in1=rstd[1][:], op0=ALU.mult, op1=ALU.mult
+                out=lift[s][:], in0=mean_var[s][:, :, 0], scalar=-1.0, in1=rstd[s][:], op0=ALU.mult, op1=ALU.mult
             )
 
         sorted_x = {}
@@ -301,7 +309,7 @@ def tile_modalityadaptivemodule_pa_k_kernel(
             xs = work.tile([P, TILES, CHUNK_GROUPS, PACK, P], F32)
             sorted_x[(s, c)] = xs
             for part, j in [(part, j) for part in range(parts) for j in range(TILES)]:
-                cut = VECTOR_SLOTS[s] if j == TILES - 1 else PACK
+                cut = PACK - 1 if j == TILES - 1 and c in SCALAR_CHUNKS[s] else PACK
                 gs = slice(part * CHUNK_GROUPS // parts, (part + 1) * CHUNK_GROUPS // parts)
                 x_sorted = x_chunks[(s, c)][:, j, :].rearrange("r (g p t) -> r g t p", p=P, t=PACK)
                 nc.vector.tensor_scalar(
@@ -315,7 +323,7 @@ def tile_modalityadaptivemodule_pa_k_kernel(
                 for u in range(cut, PACK):
                     nc.scalar.activation(
                         out=xs[:, j, gs, u, :], in_=x_sorted[:, gs, u], func=ACT.Identity,
-                        scale=rstd[s][:, j : j + 1], bias=lift[:, j : j + 1],
+                        scale=rstd[s][:, j : j + 1], bias=lift[s][:, j : j + 1],
                     )
 
         def next_chunk(s, c):
@@ -355,25 +363,26 @@ def tile_modalityadaptivemodule_pa_k_kernel(
             planes_of[r] = planes
 
         def regroup(r, first=0, last=ROUND_GROUPS):
-            if r not in grouped_of:
-                grouped = work.tile([P, ROUND_GROUPS * ROWS, PACK], BF16, align_bytes=64)
-                grouped_of[r] = grouped
+            c, part = divmod(r, ROUNDS_PER_CHUNK)
+            if part == 0 and first == 0:
+                grouped_of[c] = work.tile([P, CHUNK_GROUPS * ROWS, PACK], BF16, align_bytes=64, name="grouped")
             cols = slice(first * ROWS, last * ROWS)
+            start = part * ROUND_GROUPS * ROWS
             nc.vector.tensor_copy(
-                out=grouped_of[r][:, cols, :].rearrange("p (c i) t -> p c t i", i=4),
+                out=grouped_of[c][:, start + first * ROWS : start + last * ROWS, :].rearrange("p (c i) t -> p c t i", i=4),
                 in_=planes_of[r][:, :, cols].rearrange("p t (c i) -> p c t i", i=4),
             )
 
-        def quantise(r, first=0, last=ROUND_GROUPS):
-            if r not in codes_of:
-                codes = mx_pool.tile([P, ROUND_GROUPS * ROWS], U32, align_bytes=64)
-                code_scales = mx_pool.tile([P, ROUND_GROUPS * ROWS], U8, align_bytes=64)
-                codes_of[r] = (codes, code_scales)
+        def quantise(c, first=0, last=CHUNK_GROUPS):
+            if first == 0:
+                codes = mx_pool.tile([P, CHUNK_GROUPS * ROWS], U32, align_bytes=64)
+                code_scales = mx_pool.tile([P, CHUNK_GROUPS * ROWS], U8, align_bytes=64)
+                codes_of[c] = (codes, code_scales)
             cols = slice(first * ROWS, last * ROWS)
             nc.vector.quantize_mx(
-                out=codes_of[r][0][:, cols].bitcast(FP8X4),
-                scales=codes_of[r][1][:, cols],
-                in_=grouped_of[r][:, cols, :].rearrange("p c t -> p (c t)"),
+                out=codes_of[c][0][:, cols].bitcast(FP8X4),
+                scales=codes_of[c][1][:, cols],
+                in_=grouped_of[c][:, cols, :].rearrange("p c t -> p (c t)"),
             )
 
         def multiply(r, gls=range(ROUND_GROUPS)):
@@ -383,12 +392,14 @@ def tile_modalityadaptivemodule_pa_k_kernel(
                     acc_qk = acc_psum.tile([P, 2 * E], F32, name="acc_qk%d" % j)
                     acc_v = acc_psum.tile([P, E], F32, name="acc_v%d" % j)
                     acc_of[(s, j)] = (acc_qk, acc_v)
-            codes, code_scales = codes_of[r]
+            c, part = divmod(r, ROUNDS_PER_CHUNK)
+            codes, code_scales = codes_of[c]
             for gl in gls:
                 g = i * ROUND_GROUPS + gl
                 w_tile = w_tiles[(s, g // W_GROUPS)]
                 for j in range(TILES):
-                    tokens = slice(gl * ROWS + j * P, gl * ROWS + (j + 1) * P)
+                    first = (part * ROUND_GROUPS + gl) * ROWS + j * P
+                    tokens = slice(first, first + P)
                     for acc, cols in zip(acc_of[(s, j)], (slice(0, 2 * E), slice(2 * E, 3 * E))):
                         nc.tensor.matmul_mx(
                             out=acc[:],
@@ -413,6 +424,9 @@ def tile_modalityadaptivemodule_pa_k_kernel(
                     in_=result[:, :, i * E : (i + 1) * E],
                 )
 
+        gs_bank = turn_psum.tile([P, PACK, P], F32, tag="bank")
+        for t in range(PACK):
+            nc.tensor.transpose(gs_bank[:, t, :], gs_sorted[:, t, :], identity[:])
         UNIT_JOBS = TILES * UNIT_BLOCKS
         sum_banks = [turn_psum.tile([P, STAT_BLOCK], F32, tag="bank", name="sum_bank%d" % j) for j in range(TILES)]
         for step in range(STEPS):
@@ -420,12 +434,8 @@ def tile_modalityadaptivemodule_pa_k_kernel(
                 vector_stats(0, job)
             for j in range(TILES):
                 square(0, step, j)
-                add_up_text(step, j)
-            if step == STEPS - 3:
-                gs_bank = turn_psum.tile([P, PACK, P], F32, tag="bank")
-                for t in range(PACK):
-                    nc.tensor.transpose(gs_bank[:, t, :], gs_sorted[:, t, :], identity[:])
-            if step == STEPS - 2:
+            add_up_text(step)
+            if step == 0:
                 nc.vector.tensor_copy(out=gs_cols[:], in_=gs_bank[:])
         for s in range(STREAMS):
             nc.gpsimd.memset(w_planes[s][:].rearrange("p g n -> p (g n)").bitcast(I32), 0)
@@ -444,6 +454,7 @@ def tile_modalityadaptivemodule_pa_k_kernel(
         for job in range(HEAD_JOBS // 2, HEAD_JOBS):
             scalar_stats_img(job)
         next_chunk(0, 0)
+        lift_rows(0)
 
         STAT_ROUNDS = 13
 
@@ -456,7 +467,7 @@ def tile_modalityadaptivemodule_pa_k_kernel(
         img_steps = {
             STAT_ROUNDS: (None, None, mean_img, lambda: total_square(1)),
             STAT_ROUNDS + 1: (None, lambda: mean_offset(1), lambda: offset_excess(1), lambda: scalar_m2(1)),
-            STAT_ROUNDS + 2: (lambda: aggregate(1), lambda: invert(1), lift_img),
+            STAT_ROUNDS + 2: (lambda: aggregate(1), lambda: invert(1), lambda: lift_rows(1)),
         }
 
         def img_step(r, i):
@@ -476,11 +487,12 @@ def tile_modalityadaptivemodule_pa_k_kernel(
             if r >= 2:
                 regroup(r - 2)
             img_step(r, 1)
-            if r >= 3:
-                quantise(r - 3)
             img_step(r, 2)
-            if (r + 1) % ROUNDS_PER_CHUNK == 0 and r + 1 < ALL_ROUNDS:
-                next_chunk(*divmod((r + 1) // ROUNDS_PER_CHUNK, CHUNKS))
+            if (r + 1) % ROUNDS_PER_CHUNK == 0:
+                if r + 1 < ALL_ROUNDS:
+                    next_chunk(*divmod((r + 1) // ROUNDS_PER_CHUNK, CHUNKS))
+                if r > ROUNDS_PER_CHUNK:
+                    quantise(r // ROUNDS_PER_CHUNK - 1)
             if r - 5 == ROUNDS - 1:
                 finish(0)
             if r >= 4:
@@ -499,16 +511,16 @@ def tile_modalityadaptivemodule_pa_k_kernel(
             img_step(r, 3)
 
         last = ALL_ROUNDS - 1
+        chunk = last // ROUNDS_PER_CHUNK
         multiply(last - 3)
         regroup(last - 1)
-        quantise(last - 2)
         multiply(last - 2)
         regroup(last, 0, 1)
-        quantise(last - 1)
+        quantise(chunk, 0, 2)
         multiply(last - 1)
         regroup(last, 1, 2)
-        quantise(last, 0, 1)
+        quantise(chunk, 2, 3)
         multiply(last, [0])
-        quantise(last, 1, 2)
+        quantise(chunk, 3, 4)
         multiply(last, [1])
         finish(1)

from contextlib import ExitStack

import concourse.mybir as mybir
from concourse.masks import make_identity

F32 = mybir.dt.float32
BF16 = mybir.dt.bfloat16
I32 = mybir.dt.int32
U32 = mybir.dt.uint32
U8 = mybir.dt.uint8
FP8X4 = mybir.dt.float8_e4m3fn_x4
ACT = mybir.ActivationFunctionType
ALU = mybir.AluOpType
AXIS = mybir.AxisListType

P = 128
PACK = 4
K_PASS = P * PACK
D = 16384
E = 128
EPS = 1e-5
STREAMS = 2
TILES = 2
ROWS = TILES * P
GROUPS = D // K_PASS

CHUNK = 2048
CHUNKS = D // CHUNK
X_BUFS = 12
STAT_BLOCK = 512

UNIT = CHUNK // 2
UNITS = D // UNIT
SCALAR_UNITS = [u for u in range(UNITS - 2) if u % 2 == 1] + [UNITS - 2]
VECTOR_UNITS = [u for u in range(UNITS) if u not in SCALAR_UNITS]
UNIT_BLOCKS = UNIT // STAT_BLOCK
STEPS = len(SCALAR_UNITS)
GPSIMD_STEPS = (0, 1, 3)
GPSIMD_TAKEN = 5
TENSOR_TEXT_STEPS = [step for step in range(STEPS) if step not in GPSIMD_STEPS]
SCALAR_UNITS_IMG = [1, 3, 5, 7, 9, 11, 13]
TENSOR_BATCHES = ((0, (1, 2)), (6, (3, 4)))
TENSOR_STEPS = [step for r, steps in TENSOR_BATCHES for step in steps]
SUM_STEPS = [step for step in range(len(SCALAR_UNITS_IMG)) if step not in TENSOR_STEPS]
VECTOR_UNITS_IMG = [u for u in range(UNITS) if u not in SCALAR_UNITS_IMG]
UNITS_OF = ((VECTOR_UNITS, SCALAR_UNITS), (VECTOR_UNITS_IMG, SCALAR_UNITS_IMG))
SCALAR_COLS = [UNIT * len(scalar_units) for vector_units, scalar_units in UNITS_OF]
TUPLES = [2 * UNIT_BLOCKS * len(vector_units) for vector_units, scalar_units in UNITS_OF]
VECTOR_JOBS = [TILES * UNIT_BLOCKS * len(vector_units) for vector_units, scalar_units in UNITS_OF]
SCALAR_JOBS = [
    (square, step, j)
    for step in range(len(SCALAR_UNITS_IMG))
    for square in ((False, True) if step in SUM_STEPS else (True,))
    for j in range(TILES)
]
HEAD_JOBS = 4
HEAD_VECTOR = 4

ROUND_GROUPS = 2
ROUND_COLS = ROUND_GROUPS * K_PASS
ROUNDS = GROUPS // ROUND_GROUPS
ROUNDS_PER_CHUNK = CHUNK // ROUND_COLS
CHUNK_GROUPS = CHUNK // K_PASS
SCALAR_CHUNKS = (range(6, CHUNKS), range(CHUNKS))
W_GROUPS = 4
W_TILES = GROUPS // W_GROUPS
W_BUFS = 4
ALL_ROUNDS = STREAMS * ROUNDS
ROUNDS_PER_W = W_GROUPS // ROUND_GROUPS

FLOPS = 2 * 3 * STREAMS * ROWS * D * E


def tile_modalityadaptivemodule_pa_k_kernel(
    tc,
    text, img, ln_t_g, ln_t_b, ln_i_g, ln_i_b,
    Wq_words, Wq_scales, bq,
    Wkt_words, Wkt_scales, bkt,
    Wvt_words, Wvt_scales, bvt,
    Wki_words, Wki_scales, bki,
    Wvi_words, Wvi_scales, bvi,
    out_0, out_1, out_2,
):
    nc = tc.nc
    streams = (text, img)
    words_of = ((Wkt_words, Wq_words, Wvt_words), (Wq_words, Wki_words, Wvi_words))
    scales_of = ((Wkt_scales, Wq_scales, Wvt_scales), (Wq_scales, Wki_scales, Wvi_scales))
    outs_of = ((out_1, out_0, out_2), (out_0, out_1, out_2))

    with ExitStack() as ctx:
        const = ctx.enter_context(tc.tile_pool(name="const", bufs=1))
        x_pool = ctx.enter_context(tc.tile_pool(name="x", bufs=X_BUFS))
        w_pool = ctx.enter_context(tc.tile_pool(name="w", bufs=W_BUFS))
        work = ctx.enter_context(tc.tile_pool(name="work", bufs=2))
        mx_pool = ctx.enter_context(tc.tile_pool(name="mx", bufs=2))
        turn_psum = ctx.enter_context(tc.psum_pool(name="turn", bufs=4))
        acc_psum = ctx.enter_context(tc.psum_pool(name="acc", bufs=1))
        ctx.enter_context(tc.manual_schedule())

        eps = const.tile([P, 1], F32)
        nc.vector.memset(eps[:], EPS)
        warm = const.tile([P, 1], F32)
        nc.scalar.activation(out=warm[:], in_=eps[:], func=ACT.Sqrt)

        x_chunks = {}

        def load_x(s, c, pieces=1):
            x_chunk = x_pool.tile([P, TILES, CHUNK], BF16)
            width = CHUNK // pieces
            for i in range(pieces):
                if (s, c, i) == (0, 0, 1):
                    load_gains()
                nc.sync.dma_start(
                    out=x_chunk[:, :, i * width : (i + 1) * width],
                    in_=streams[s].rearrange("b r d -> r b d")[:, :, c * CHUNK + i * width : c * CHUNK + (i + 1) * width],
                )
            x_chunks[(s, c)] = x_chunk

        w_tiles = {}

        def load_weights(s, h):
            w_tile = w_pool.tile([P, W_GROUPS, 3 * E], U32, align_bytes=64)
            for i, words in enumerate(words_of[s]):
                nc.sync.dma_start(
                    out=w_tile[:, :, i * E : (i + 1) * E].bitcast(I32),
                    in_=words[h * W_GROUPS : (h + 1) * W_GROUPS]
                    .rearrange("g p n t -> p g (n t)")
                    .bitcast(I32),
                )
            w_tiles[(s, h)] = w_tile

        w_planes = [const.tile([P, GROUPS, 3 * E], U8, align_bytes=64, name="w_plane%d" % s) for s in range(STREAMS)]

        def load_scale_planes(s):
            for i, scales in enumerate(scales_of[s]):
                for quad in range(4):
                    nc.sync.dma_start(
                        out=w_planes[s][32 * quad : 32 * quad + 4, :, i * E : (i + 1) * E].bitcast(I32),
                        in_=scales[:, 4 * quad : 4 * quad + 4, :]
                        .rearrange("g r n -> r g n")
                        .bitcast(I32),
                    )

        bias = const.tile([P, 5 * E], BF16)
        pair_bias = (bias[:, 0 : 2 * E], bias[:, E : 3 * E])
        v_bias = (bias[:, 3 * E : 4 * E], bias[:, 4 * E : 5 * E])

        def load_biases():
            for slot, vector in enumerate((bkt, bq, bki, bvt, bvi)):
                nc.sync.dma_start(out=bias[:, slot * E : (slot + 1) * E], in_=vector.partition_broadcast(P))

        gs_rows = const.tile([P, K_PASS], BF16)

        def load_gains():
            for v, vector in enumerate((ln_t_g, ln_t_b, ln_i_g, ln_i_b)):
                nc.sync.dma_start(
                    out=gs_rows[v * GROUPS : (v + 1) * GROUPS, :],
                    in_=vector.rearrange("(g c) -> g c", c=K_PASS),
                )

        identity = const.tile([P, P], F32)
        make_identity(nc, identity[:])
        identity_bf = const.tile([P, P], BF16)
        nc.gpsimd.tensor_copy(out=identity_bf[:], in_=identity[:])

        for c in range(CHUNKS):
            load_x(0, c, pieces=2 if c in (0, CHUNKS - 1) else 1)
        for c in range(X_BUFS - CHUNKS):
            load_x(1, c)

        gs_sorted = const.tile([P, PACK, P], F32)
        nc.scalar.copy(out=gs_sorted[:], in_=gs_rows[:].rearrange("q (p t) -> q t p", t=PACK))
        gs_cols = const.tile([P, PACK, P], F32)

        tuples = [const.tile([P, TILES, TUPLES[s] + 1, 3], F32, name="tuples%d" % s) for s in range(STREAMS)]
        squares = [const.tile([P, TILES, len(UNITS_OF[s][1])], F32, name="squares%d" % s) for s in range(STREAMS)]
        sums = const.tile([P, TILES, len(SUM_STEPS) + len(TENSOR_BATCHES)], F32)
        gpsimd_sums = [const.tile([P, STAT_BLOCK], F32, name="gpsimd_sum%d" % j) for j in range(TILES)]
        offset = [const.tile([P, TILES], F32, name="offset%d" % s) for s in range(STREAMS)]
        excess = [const.tile([P, TILES], F32, name="excess%d" % s) for s in range(STREAMS)]
        square_sum = [const.tile([P, TILES], F32, name="square_sum%d" % s) for s in range(STREAMS)]
        mean_var = [const.tile([P, TILES, 2], F32, name="mean_var%d" % s) for s in range(STREAMS)]
        std = [const.tile([P, TILES], F32, name="std%d" % s) for s in range(STREAMS)]
        rstd = [const.tile([P, TILES], F32, name="rstd%d" % s) for s in range(STREAMS)]
        lift = [const.tile([P, TILES], F32, name="lift%d" % s) for s in range(STREAMS)]

        for s in range(STREAMS):
            nc.vector.memset(tuples[s][:, :, TUPLES[s], 0], float(SCALAR_COLS[s]))

        def unit_rows(s, unit, j):
            c, half = divmod(unit, 2)
            return x_chunks[(s, c)][:, j, half * UNIT : (half + 1) * UNIT]

        def vector_stats(s, job):
            block, j = divmod(job, TILES)
            step, b = divmod(block, UNIT_BLOCKS)
            nc.vector.bn_stats(
                out=tuples[s][:, j, 2 * block : 2 * block + 2, :].rearrange("p a b -> p (a b)"),
                in_=unit_rows(s, UNITS_OF[s][0][step], j)[:, b * STAT_BLOCK : (b + 1) * STAT_BLOCK],
            )

        def square(s, step, j):
            unread = work.tile([P, UNIT], BF16)
            nc.scalar.activation(
                out=unread[:], in_=unit_rows(s, UNITS_OF[s][1][step], j), func=ACT.Square,
                bias=tuples[s][:, j, 0, 1:2], scale=-1.0, accum_out=squares[s][:, j, step : step + 1],
            )

        def add_up(s, step, j):
            unread = work.tile([P, UNIT], BF16)
            nc.scalar.activation(
                out=unread[:], in_=unit_rows(s, UNITS_OF[s][1][step], j), func=ACT.Identity,
                scale=1.0 / SCALAR_COLS[s], accum_out=sums[:, j, SUM_STEPS.index(step) : SUM_STEPS.index(step) + 1],
            )

        def add_up_text(step):
            for b in range(UNIT_BLOCKS):
                for j in range(TILES):
                    rows = unit_rows(0, SCALAR_UNITS[step], j)
                    block = rows[:, b * STAT_BLOCK : (b + 1) * STAT_BLOCK]
                    if step not in GPSIMD_STEPS:
                        first = step == TENSOR_TEXT_STEPS[0] and b == 0
                        last = step == STEPS - 1 and b == UNIT_BLOCKS - 1
                        nc.tensor.matmul(sum_banks[j][:], lhsT=identity_bf[:], rhs=block, start=first, stop=last)
                    elif step > GPSIMD_STEPS[0]:
                        nc.gpsimd.tensor_tensor(out=gpsimd_sums[j][:], in0=gpsimd_sums[j][:], in1=block, op=ALU.add)
                    elif b == 1:
                        nc.gpsimd.tensor_tensor(out=gpsimd_sums[j][:], in0=rows[:, :STAT_BLOCK], in1=block, op=ALU.add)
            if step == GPSIMD_TAKEN:
                for j in range(TILES):
                    nc.tensor.matmul(sum_banks[j][:], lhsT=identity[:], rhs=gpsimd_sums[j][:], start=False, stop=False)

        def mean_text():
            for j in range(TILES):
                unread = work.tile([P, UNIT], BF16)
                nc.scalar.activation(
                    out=unread[:, 0:STAT_BLOCK], in_=sum_banks[j][:], func=ACT.Identity, scale=1.0 / SCALAR_COLS[0],
                    accum_out=tuples[0][:, j, TUPLES[0], 1:2],
                )

        HALF = STAT_BLOCK // 2
        batch_banks = {}

        def add_up_batch(batch):
            steps = TENSOR_BATCHES[batch][1]
            batch_bank = turn_psum.tile([P, TILES, HALF], F32, tag="bank")
            batch_banks[batch] = batch_bank
            for j in range(TILES):
                for step in steps:
                    rows = unit_rows(1, SCALAR_UNITS_IMG[step], j)
                    for b in range(UNIT // HALF):
                        nc.tensor.matmul(
                            batch_bank[:, j, :], lhsT=identity_bf[:], rhs=rows[:, b * HALF : (b + 1) * HALF],
                            start=(step == steps[0] and b == 0), stop=(step == steps[-1] and b == UNIT // HALF - 1),
                        )

        def mean_batch(batch):
            for j in range(TILES):
                unread = work.tile([P, UNIT], BF16)
                nc.scalar.activation(
                    out=unread[:, 0:HALF], in_=batch_banks[batch][:, j, :], func=ACT.Identity, scale=1.0 / SCALAR_COLS[1],
                    accum_out=sums[:, j, len(SUM_STEPS) + batch : len(SUM_STEPS) + batch + 1],
                )

        def scalar_stats_img(job):
            squared, step, j = SCALAR_JOBS[job]
            (square if squared else add_up)(1, step, j)

        def mean_img():
            nc.vector.tensor_reduce(
                out=tuples[1][:, :, TUPLES[1], 1], in_=sums[:], axis=AXIS.X, op=ALU.add
            )

        def mean_offset(s):
            nc.vector.tensor_tensor(out=offset[s][:], in0=tuples[s][:, :, TUPLES[s], 1], in1=tuples[s][:, :, 0, 1], op=ALU.subtract)

        def offset_excess(s):
            nc.vector.scalar_tensor_tensor(
                out=excess[s][:], in0=offset[s][:], scalar=float(SCALAR_COLS[s]), in1=offset[s][:], op0=ALU.mult, op1=ALU.mult
            )

        def total_square(s):
            nc.vector.tensor_reduce(out=square_sum[s][:], in_=squares[s][:], axis=AXIS.X, op=ALU.add)

        def scalar_m2(s):
            nc.vector.tensor_tensor(out=tuples[s][:, :, TUPLES[s], 2], in0=square_sum[s][:], in1=excess[s][:], op=ALU.subtract)

        def aggregate(s):
            for j in range(TILES):
                nc.vector.bn_aggr(out=mean_var[s][:, j, :], in_=tuples[s][:, j, :, :].rearrange("p n c -> p (n c)"))
            nc.scalar.activation(out=std[s][:], in_=mean_var[s][:, :, 1], func=ACT.Sqrt, bias=eps[:, 0:1], scale=1.0)

        def invert(s):
            nc.vector.reciprocal(out=rstd[s][:], in_=std[s][:])

        def lift_rows(s):
            nc.vector.scalar_tensor_tensor(
                out=lift[s][:], in0=mean_var[s][:, :, 0], scalar=-1.0, in1=rstd[s][:], op0=ALU.mult, op1=ALU.mult
            )

        sorted_x = {}
        banks = {}
        planes_of = {}
        grouped_of = {}
        codes_of = {}
        acc_of = {}

        def normalise(s, c, parts=1):
            xs = work.tile([P, TILES, CHUNK_GROUPS, PACK, P], F32)
            sorted_x[(s, c)] = xs
            for part, j in [(part, j) for part in range(parts) for j in range(TILES)]:
                cut = PACK - 1 if j == TILES - 1 and c in SCALAR_CHUNKS[s] else PACK
                gs = slice(part * CHUNK_GROUPS // parts, (part + 1) * CHUNK_GROUPS // parts)
                x_sorted = x_chunks[(s, c)][:, j, :].rearrange("r (g p t) -> r g t p", p=P, t=PACK)
                nc.vector.tensor_scalar(
                    out=xs[:, j, gs, 0:cut, :],
                    in0=x_sorted[:, gs, 0:cut],
                    scalar1=mean_var[s][:, j, 0:1],
                    scalar2=rstd[s][:, j : j + 1],
                    op0=ALU.subtract,
                    op1=ALU.mult,
                )
                for u in range(cut, PACK):
                    nc.scalar.activation(
                        out=xs[:, j, gs, u, :], in_=x_sorted[:, gs, u], func=ACT.Identity,
                        scale=rstd[s][:, j : j + 1], bias=lift[s][:, j : j + 1],
                    )

        def next_chunk(s, c):
            normalise(s, c, parts=2 if (s, c) == (0, 0) else 1)
            if s == 0 and c + X_BUFS < STREAMS * CHUNKS:
                load_x(1, c + X_BUFS - CHUNKS)

        def turn(r):
            s, i = divmod(r, ROUNDS)
            c, part = divmod(i, ROUNDS_PER_CHUNK)
            xs = sorted_x[(s, c)]
            for gl in range(ROUND_GROUPS):
                for half in range(PACK // 2):
                    bank = turn_psum.tile([P, 2, ROWS], F32, tag="bank")
                    for u in range(2):
                        for j in range(TILES):
                            nc.tensor.transpose(
                                bank[:, u, j * P : (j + 1) * P],
                                xs[:, j, part * ROUND_GROUPS + gl, 2 * half + u, :],
                                identity[:],
                            )
                    banks[(r, gl, half)] = bank

        def gain_shift(r):
            s, i = divmod(r, ROUNDS)
            planes = work.tile([P, PACK, ROUND_GROUPS * ROWS], BF16, bufs=3)
            for gl in range(ROUND_GROUPS):
                g = i * ROUND_GROUPS + gl
                for t in range(PACK):
                    nc.scalar.activation(
                        out=planes[:, t, gl * ROWS : (gl + 1) * ROWS],
                        in_=banks[(r, gl, t // 2)][:, t % 2, :],
                        func=ACT.Identity,
                        scale=gs_cols[:, t, 2 * s * GROUPS + g : 2 * s * GROUPS + g + 1],
                        bias=gs_cols[:, t, (2 * s + 1) * GROUPS + g : (2 * s + 1) * GROUPS + g + 1],
                    )
            planes_of[r] = planes

        def regroup(r, first=0, last=ROUND_GROUPS):
            c, part = divmod(r, ROUNDS_PER_CHUNK)
            if part == 0 and first == 0:
                grouped_of[c] = work.tile([P, CHUNK_GROUPS * ROWS, PACK], BF16, align_bytes=64, name="grouped")
            cols = slice(first * ROWS, last * ROWS)
            start = part * ROUND_GROUPS * ROWS
            nc.vector.tensor_copy(
                out=grouped_of[c][:, start + first * ROWS : start + last * ROWS, :].rearrange("p (c i) t -> p c t i", i=4),
                in_=planes_of[r][:, :, cols].rearrange("p t (c i) -> p c t i", i=4),
            )

        def quantise(c, first=0, last=CHUNK_GROUPS):
            if first == 0:
                codes = mx_pool.tile([P, CHUNK_GROUPS * ROWS], U32, align_bytes=64)
                code_scales = mx_pool.tile([P, CHUNK_GROUPS * ROWS], U8, align_bytes=64)
                codes_of[c] = (codes, code_scales)
            cols = slice(first * ROWS, last * ROWS)
            nc.vector.quantize_mx(
                out=codes_of[c][0][:, cols].bitcast(FP8X4),
                scales=codes_of[c][1][:, cols],
                in_=grouped_of[c][:, cols, :].rearrange("p c t -> p (c t)"),
            )

        def multiply(r, gls=range(ROUND_GROUPS)):
            s, i = divmod(r, ROUNDS)
            if i == 0:
                for j in range(TILES):
                    acc_qk = acc_psum.tile([P, 2 * E], F32, name="acc_qk%d" % j)
                    acc_v = acc_psum.tile([P, E], F32, name="acc_v%d" % j)
                    acc_of[(s, j)] = (acc_qk, acc_v)
            c, part = divmod(r, ROUNDS_PER_CHUNK)
            codes, code_scales = codes_of[c]
            for gl in gls:
                g = i * ROUND_GROUPS + gl
                w_tile = w_tiles[(s, g // W_GROUPS)]
                for j in range(TILES):
                    first = (part * ROUND_GROUPS + gl) * ROWS + j * P
                    tokens = slice(first, first + P)
                    for acc, cols in zip(acc_of[(s, j)], (slice(0, 2 * E), slice(2 * E, 3 * E))):
                        nc.tensor.matmul_mx(
                            out=acc[:],
                            lhsT=codes[:, tokens].bitcast(FP8X4),
                            lhsT_scale=code_scales[:, tokens],
                            rhs=w_tile[:, g % W_GROUPS, cols].bitcast(FP8X4),
                            rhs_scale=w_planes[s][:, g, cols],
                            start=(g == 0),
                            stop=(g == GROUPS - 1),
                        )

        def finish(s):
            result = work.tile([P, TILES, 3 * E], F32)
            for j in range(TILES):
                acc_qk, acc_v = acc_of[(s, j)]
                nc.vector.tensor_tensor(out=result[:, j, 0 : 2 * E], in0=acc_qk[:], in1=pair_bias[s], op=ALU.add)
                nc.vector.tensor_tensor(out=result[:, j, 2 * E :], in0=acc_v[:], in1=v_bias[s], op=ALU.add)
            for i, out in enumerate(outs_of[s]):
                queue = nc.scalar if s == 1 and i == 1 else nc.sync
                queue.dma_start(
                    out=out[TILES * s : TILES * (s + 1)].rearrange("b r n -> r b n"),
                    in_=result[:, :, i * E : (i + 1) * E],
                )

        gs_bank = turn_psum.tile([P, PACK, P], F32, tag="bank")
        for t in range(PACK):
            nc.tensor.transpose(gs_bank[:, t, :], gs_sorted[:, t, :], identity[:])
        UNIT_JOBS = TILES * UNIT_BLOCKS
        sum_banks = [turn_psum.tile([P, STAT_BLOCK], F32, tag="bank", name="sum_bank%d" % j) for j in range(TILES)]
        for step in range(STEPS):
            for job in range(step * UNIT_JOBS, (step + 1) * UNIT_JOBS):
                vector_stats(0, job)
            for j in range(TILES):
                square(0, step, j)
            add_up_text(step)
            if step == 0:
                nc.vector.tensor_copy(out=gs_cols[:], in_=gs_bank[:])
        for s in range(STREAMS):
            nc.gpsimd.memset(w_planes[s][:].rearrange("p g n -> p (g n)").bitcast(I32), 0)
        load_scale_planes(0)
        for h in range(W_BUFS):
            load_weights(0, h)
        mean_text()
        text_steps = [total_square, mean_offset, offset_excess, scalar_m2]
        for job in range(HEAD_VECTOR):
            text_steps[job](0)
            vector_stats(1, job)
        for job in range(HEAD_JOBS // 2):
            scalar_stats_img(job)
        aggregate(0)
        invert(0)
        for job in range(HEAD_JOBS // 2, HEAD_JOBS):
            scalar_stats_img(job)
        next_chunk(0, 0)
        lift_rows(0)

        STAT_ROUNDS = 13

        def first_vector(r):
            return HEAD_VECTOR + r * (VECTOR_JOBS[1] - HEAD_VECTOR) // STAT_ROUNDS

        def first_scalar(r):
            return HEAD_JOBS + r * (len(SCALAR_JOBS) - HEAD_JOBS) // STAT_ROUNDS

        img_steps = {
            STAT_ROUNDS: (None, None, mean_img, lambda: total_square(1)),
            STAT_ROUNDS + 1: (None, lambda: mean_offset(1), lambda: offset_excess(1), lambda: scalar_m2(1)),
            STAT_ROUNDS + 2: (lambda: aggregate(1), lambda: invert(1), lambda: lift_rows(1)),
        }

        def img_step(r, i):
            steps = img_steps.get(r, ())
            if i < len(steps) and steps[i]:
                steps[i]()

        for r in range(ALL_ROUNDS):
            img_step(r, 0)
            turn(r)
            gain_shift(r)
            for batch in range(len(TENSOR_BATCHES)):
                if r == TENSOR_BATCHES[batch][0]:
                    add_up_batch(batch)
                if r == TENSOR_BATCHES[batch][0] + 1:
                    mean_batch(batch)
            if r >= 2:
                regroup(r - 2)
            img_step(r, 1)
            img_step(r, 2)
            if (r + 1) % ROUNDS_PER_CHUNK == 0:
                if r + 1 < ALL_ROUNDS:
                    next_chunk(*divmod((r + 1) // ROUNDS_PER_CHUNK, CHUNKS))
                if r > ROUNDS_PER_CHUNK:
                    quantise(r // ROUNDS_PER_CHUNK - 1)
            if r - 5 == ROUNDS - 1:
                finish(0)
            if r >= 4:
                multiply(r - 4)
                h = (r - 4) // ROUNDS_PER_W + W_BUFS
                if (r - 4) % ROUNDS_PER_W == ROUNDS_PER_W - 1 and h < STREAMS * W_TILES:
                    load_weights(h // W_TILES, h % W_TILES)
            if r < STAT_ROUNDS:
                for job in range(first_vector(r), first_vector(r + 1)):
                    vector_stats(1, job)
                for job in range(first_scalar(r), first_scalar(r + 1)):
                    scalar_stats_img(job)
            if r == STAT_ROUNDS - 1:
                load_scale_planes(1)
                load_biases()
            img_step(r, 3)

        last = ALL_ROUNDS - 1
        chunk = last // ROUNDS_PER_CHUNK
        multiply(last - 3)
        regroup(last - 1)
        multiply(last - 2)
        regroup(last, 0, 1)
        quantise(chunk, 0, 2)
        multiply(last - 1)
        regroup(last, 1, 2)
        quantise(chunk, 2, 3)
        multiply(last, [0])
        quantise(chunk, 3, 4)
        multiply(last, [1])
        finish(1)
